import numpy as np
import ml_dtypes


def mxq(x, axis, fmt="e4m3"):
    dtype, down = {"e4m3": (ml_dtypes.float8_e4m3fn, 7), "e5m2": (ml_dtypes.float8_e5m2, 14)}[fmt]
    v = np.moveaxis(np.asarray(x, np.float32).astype(ml_dtypes.bfloat16).astype(np.float64), axis, -1)
    blocks = v.reshape(v.shape[:-1] + (-1, 32))
    amax = np.abs(blocks).max(-1, keepdims=True)
    byte = np.maximum(np.where(amax > 0, np.frexp(amax)[1] - 1 + 127, 0) - down, 1)
    scale = np.exp2(byte - 127.0)
    codes = (blocks / scale).astype(np.float32).astype(dtype).astype(np.float64)
    return np.moveaxis((codes * scale).reshape(v.shape), -1, axis)


WIDE = False


def mx_kscale(k):
    if not WIDE:
        return np.ones(k)
    levels = np.array([10, -10, 5, -5, 0])
    a = np.random.permutation(np.resize(levels, k // 512 * 4)).reshape(k // 512, 4)
    idx = np.arange(k)
    return np.exp2(a[idx // 512, idx % 128 // 32])


BF16 = ml_dtypes.bfloat16


def bf(x):
    return np.asarray(x, np.float32).astype(BF16)


def f64(x):
    return np.asarray(x).astype(np.float64)


B, S, DV, DL, D = 2, 512, 1024, 1024, 1024
EPS = 1e-5
TEMPERATURE = 0.07


def layernorm(x, g, b):
    m = x.mean(-1, keepdims=True)
    v = np.square(x - m).mean(-1, keepdims=True)
    return (x - m) / np.sqrt(v + EPS) * g + b


def setup_inputs():
    s, u = mx_kscale(DV), mx_kscale(DL)
    return {
        'vision_features': bf(np.random.standard_normal((B, S, DV)) * s),
        'language_features': bf(np.random.standard_normal((B, S, DL)) * u),
        'vW': bf(np.random.standard_normal((DV, D)) / np.sqrt(DV) / s[:, None]),
        'vb': bf(0.1 * np.random.standard_normal(D)),
        'vg': bf(1.0 + 0.1 * np.random.standard_normal(D)),
        'vbeta': bf(0.1 * np.random.standard_normal(D)),
        'lW': bf(np.random.standard_normal((DL, D)) / np.sqrt(DL) / u[:, None]),
        'lb': bf(0.1 * np.random.standard_normal(D)),
        'lg': bf(1.0 + 0.1 * np.random.standard_normal(D)),
        'lbeta': bf(0.1 * np.random.standard_normal(D)),
        'claw': bf((np.random.standard_normal((D, D)) + 0.15) / np.sqrt(D)),
    }


def reference(vision_features, language_features, vW, vb, vg, vbeta, lW, lb, lg, lbeta, claw):
    hv = (mxq(f64(vision_features), 2, 'e4m3') @ mxq(f64(vW), 0, 'e4m3')) + f64(vb)
    vp = np.maximum(layernorm(hv, f64(vg), f64(vbeta)), 0.0)
    hl = (mxq(f64(language_features), 2, 'e4m3') @ mxq(f64(lW), 0, 'e4m3')) + f64(lb)
    lp = np.maximum(layernorm(hl, f64(lg), f64(lbeta)), 0.0)
    sim = (mxq(vp, 2, 'e4m3') @ mxq(lp, 2, 'e4m3').transpose(0, 2, 1)) * (f64(claw).mean() / TEMPERATURE)
    e = np.exp(sim - sim.max(-1, keepdims=True))
    return e / e.sum(-1, keepdims=True)

@@ -1,0 +1,406 @@
+from contextlib import ExitStack
+
+import concourse.mybir as mybir
+from concourse.masks import make_identity
+
+F32 = mybir.dt.float32
+BF16 = mybir.dt.bfloat16
+U32 = mybir.dt.uint32
+U8 = mybir.dt.uint8
+FP8X4 = mybir.dt.float8_e4m3fn_x4
+ALU = mybir.AluOpType
+ACT = mybir.ActivationFunctionType
+AX = mybir.AxisListType
+
+P = 128
+PACK = 4
+K_PASS = P * PACK
+BANK = 512
+
+BATCHES, TOKENS, D = 2, 512, 1024
+EPS = 1e-5
+TEMPERATURE = 0.07
+PASSES = D // K_PASS
+HALVES = D // BANK
+CHUNKS = D // P
+RUN = 4
+
+LANG, VIS = 0, 1
+UNITS = 2 * BATCHES
+TILES_PER_UNIT = TOKENS // P
+N_TILES = UNITS * TILES_PER_UNIT
+CHUNKS_PER_STEP = CHUNKS // TILES_PER_UNIT
+AHEAD = 2
+ROWS_FROM = TILES_PER_UNIT + 1
+STEPS = N_TILES + TILES_PER_UNIT + ROWS_FROM + 1
+CLAW_STEP = 2 * TILES_PER_UNIT
+
+FLOPS = 2 * 2 * BATCHES * TOKENS * D * D + 2 * BATCHES * TOKENS * TOKENS * D
+
+
+def tile_clawmatrix_pa_kernel(
+    tc, vision_features, language_features, vW, vb, vg, vbeta, lW, lb, lg, lbeta, claw, out
+):
+    nc = tc.nc
+    features = (language_features.flatten_outer_dims(), vision_features.flatten_outer_dims())
+    weights = (lW, vW)
+    biases = (lb, vb)
+    gains = (lg, vg)
+    shifts = (lbeta, vbeta)
+    out_rows = out.flatten_outer_dims()
+
+    with ExitStack() as ctx:
+        const = ctx.enter_context(tc.tile_pool(name="const", bufs=1))
+        resident = ctx.enter_context(tc.tile_pool(name="resident", bufs=1))
+        grouped_pool = ctx.enter_context(tc.tile_pool(name="grouped", bufs=4))
+        token_pool = ctx.enter_context(tc.tile_pool(name="tokens", bufs=4))
+        row_pool = ctx.enter_context(tc.tile_pool(name="rows", bufs=2 * TILES_PER_UNIT + 1))
+        scrap_pool = ctx.enter_context(tc.tile_pool(name="scrap", bufs=1))
+        act_pool = ctx.enter_context(tc.tile_pool(name="act", bufs=2))
+        prob_pool = ctx.enter_context(tc.tile_pool(name="probs", bufs=3))
+        stat_pool = ctx.enter_context(tc.tile_pool(name="stats", bufs=4))
+        x_psum = ctx.enter_context(tc.psum_pool(name="x_psum", bufs=1))
+        h_psum = ctx.enter_context(tc.psum_pool(name="h_psum", bufs=4))
+        y_psum = ctx.enter_context(tc.psum_pool(name="y_psum", bufs=2))
+        s_psum = ctx.enter_context(tc.psum_pool(name="s_psum", bufs=1))
+
+        ident_f32 = const.tile([P, P], F32)
+        make_identity(nc, ident_f32[:])
+        ident_bf16 = const.tile([P, P], BF16)
+        nc.vector.tensor_copy(out=ident_bf16[:], in_=ident_f32[:])
+        ones_bf16 = const.tile([P, P], BF16)
+        nc.vector.memset(ones_bf16[:], 1.0)
+        minus_half = const.tile([P, 1], F32)
+        nc.vector.memset(minus_half[:], -0.5)
+        warm = const.tile([P, 1], F32)
+        nc.vector.memset(warm[:], 0.0)
+        nc.scalar.activation(out=warm[:], in_=warm[:], func=ACT.Exp)
+
+        bias_rows = const.tile([P, 2, D], BF16)
+        nc.vector.memset(bias_rows[:], 0.0)
+        for s in (LANG, VIS):
+            nc.sync.dma_start(
+                out=bias_rows[0:1, s, :], in_=biases[s].rearrange("(o d) -> o d", o=1)
+            )
+
+        def load_tokens(u):
+            s, b = u % 2, u // 2
+            x_unit = resident.tile([P, TILES_PER_UNIT, D], BF16, name="x_unit%d" % u)
+            nc.sync.dma_start(
+                out=x_unit[:],
+                in_=features[s][b * TOKENS : (b + 1) * TOKENS, :].rearrange(
+                    "(n p) k -> p n k", p=P
+                ),
+            )
+            return x_unit
+
+        def load_weights(s):
+            w_rows = resident.tile([P, PASSES, PACK, D], BF16, name="w_rows%d" % s)
+            for g in range(PASSES):
+                nc.sync.dma_start(
+                    out=w_rows[:, g, :, :].rearrange("q (u e) d -> q u e d", u=2),
+                    in_=weights[s][g * K_PASS : (g + 1) * K_PASS, :].rearrange(
+                        "(u q e) d -> q u e d", u=2, e=2
+                    ),
+                )
+            return w_rows
+
+        x_units = [None] * UNITS
+        w_rows = [None] * 2
+        x_units[0] = load_tokens(0)
+        w_rows[LANG] = load_weights(LANG)
+        affine_rows = const.tile([P, P], BF16)
+        nc.vector.memset(affine_rows[:], 0.0)
+        for s in (LANG, VIS):
+            for v, vector in enumerate((gains[s], shifts[s])):
+                first = (2 * s + v) * CHUNKS
+                nc.sync.dma_start(
+                    out=affine_rows[first : first + CHUNKS, :],
+                    in_=vector.rearrange("(c p) -> c p", p=P),
+                )
+        x_units[1] = load_tokens(1)
+        w_rows[VIS] = load_weights(VIS)
+        x_units[2] = load_tokens(2)
+        x_units[3] = load_tokens(3)
+        claw_sb = resident.tile([P, D * D // P], BF16)
+        nc.sync.dma_start(out=claw_sb[:], in_=claw.rearrange("(p r) c -> p (r c)", p=P))
+
+        w_codes, w_scales, a_codes, a_scales = [], [], [], []
+        for s in (LANG, VIS):
+            wc = resident.tile([P, PASSES, D], U32, name="w_codes%d" % s, align_bytes=64)
+            ws = resident.tile([P, PASSES, D], U8, name="w_scales%d" % s, align_bytes=64)
+            w_codes.append(wc)
+            w_scales.append(ws)
+        for u in range(UNITS):
+            ac = resident.tile([P, PASSES, TOKENS], U32, name="a_codes%d" % u, align_bytes=64)
+            asc = resident.tile([P, PASSES, TOKENS], U8, name="a_scales%d" % u, align_bytes=64)
+            a_codes.append(ac)
+            a_scales.append(asc)
+
+        def regroup_weights(s, g, half, engine):
+            cols = slice(half * BANK, (half + 1) * BANK)
+            grouped = grouped_pool.tile([P, BANK, PACK], BF16, tag="grouped", align_bytes=64)
+            dst = grouped[:].rearrange("p (c i) t -> p c t i", i=RUN)
+            src = w_rows[s][:, g, :, cols].rearrange("p t (c i) -> p c t i", i=RUN)
+            if engine == "vector":
+                nc.vector.tensor_copy(out=dst, in_=src)
+            else:
+                nc.scalar.copy(out=dst, in_=src)
+            return grouped
+
+        def quantise_weights(s, g, half, grouped):
+            cols = slice(half * BANK, (half + 1) * BANK)
+            nc.vector.quantize_mx(
+                out=w_codes[s][:, g, cols].bitcast(FP8X4),
+                scales=w_scales[s][:, g, cols],
+                in_=grouped[:].rearrange("p d t -> p (d t)"),
+            )
+
+        def prepare_tokens(i):
+            u, n = divmod(i, TILES_PER_UNIT)
+            words = x_units[u][:, n, :].bitcast(F32)
+            xT = x_psum.tile([P, PACK, P], F32, tag="xT")
+            for q in range(PACK):
+                nc.tensor.transpose(
+                    out=xT[:, q, :], in_=words[:, q * P : (q + 1) * P], identity=ident_f32[:]
+                )
+            x_grouped = token_pool.tile([P, PASSES, P, 2], F32, tag="x_grouped", align_bytes=64)
+            nc.scalar.copy(out=x_grouped[:], in_=xT[:].rearrange("p (g u) t -> p g t u", u=2))
+            return x_grouped
+
+        def quantise_tokens(x_grouped):
+            x_codes = token_pool.tile([P, PASSES * P], U32, tag="x_codes", align_bytes=64)
+            x_scales = token_pool.tile([P, PASSES * P], U8, tag="x_scales", align_bytes=64)
+            nc.vector.quantize_mx(
+                out=x_codes[:].bitcast(FP8X4),
+                scales=x_scales[:],
+                in_=x_grouped[:].rearrange("p g t u -> p (g t u)").bitcast(BF16),
+            )
+            return x_codes, x_scales
+
+        def project(i, x_codes, x_scales):
+            s = (i // TILES_PER_UNIT) % 2
+            h = row_pool.tile([P, D], F32, tag="h")
+            sums = stat_pool.tile([P, HALVES], F32, tag="sums")
+            for half in range(HALVES):
+                cols = slice(half * BANK, (half + 1) * BANK)
+                acc = h_psum.tile([P, BANK], F32, tag="acc")
+                for g in range(PASSES):
+                    toks = slice(g * P, (g + 1) * P)
+                    nc.tensor.matmul_mx(
+                        out=acc[:],
+                        lhsT=x_codes[:, toks].bitcast(FP8X4),
+                        lhsT_scale=x_scales[:, toks],
+                        rhs=w_codes[s][:, g, cols].bitcast(FP8X4),
+                        rhs_scale=w_scales[s][:, g, cols],
+                        start=(g == 0),
+                        stop=(g == PASSES - 1),
+                    )
+                nc.vector.scalar_tensor_tensor(
+                    out=h[:, cols],
+                    in0=acc[:],
+                    scalar=1.0,
+                    in1=bias_all[:, s, cols],
+                    op0=ALU.mult,
+                    op1=ALU.add,
+                    accum_out=sums[:, half : half + 1],
+                )
+            neg_mean = stat_pool.tile([P, 1], F32, tag="neg_mean")
+            nc.vector.tensor_scalar(
+                out=neg_mean[:],
+                in0=sums[:, 0:1],
+                scalar1=sums[:, 1:2],
+                scalar2=-1.0 / D,
+                op0=ALU.add,
+                op1=ALU.mult,
+            )
+            return h, neg_mean
+
+        def squared_deviations(h, neg_mean):
+            scrap = scrap_pool.tile([P, D], BF16, tag="scrap")
+            ssq = stat_pool.tile([P, 1], F32, tag="ssq")
+            nc.scalar.activation(
+                out=scrap[:], in_=h[:], func=ACT.Square, bias=neg_mean[:], scale=1.0,
+                accum_out=ssq[:],
+            )
+            return ssq
+
+        def normalise(h, neg_mean, ssq):
+            var_eps = stat_pool.tile([P, 1], F32, tag="var_eps")
+            nc.gpsimd.tensor_scalar(
+                out=var_eps[:], in0=ssq[:], scalar1=1.0 / D, scalar2=EPS,
+                op0=ALU.mult, op1=ALU.add,
+            )
+            rstd = stat_pool.tile([P, 1], F32, tag="rstd")
+            nc.gpsimd.tensor_tensor(out=rstd[:], in0=var_eps[:], in1=minus_half[:], op=ALU.pow)
+            nc.vector.tensor_scalar(
+                out=h[:], in0=h[:], scalar1=neg_mean[:], scalar2=rstd[:],
+                op0=ALU.add, op1=ALU.mult,
+            )
+
+        def transpose_features(u, c, act):
+            s = u % 2
+            yT = y_psum.tile([P, TOKENS], F32, tag="yT")
+            for n in range(TILES_PER_UNIT):
+                nc.tensor.transpose(
+                    out=yT[:, n * P : (n + 1) * P],
+                    in_=normalised[u * TILES_PER_UNIT + n][:, c * P : (c + 1) * P],
+                    identity=ident_f32[:],
+                )
+            gain = affine[:, 2 * s * CHUNKS + c : 2 * s * CHUNKS + c + 1]
+            shift = affine[:, (2 * s + 1) * CHUNKS + c : (2 * s + 1) * CHUNKS + c + 1]
+            nc.scalar.activation(
+                out=act[:, c % PACK, :], in_=yT[:], func=ACT.Identity, scale=gain, bias=shift
+            )
+
+        def regroup_features(act):
+            grouped = grouped_pool.tile([P, TOKENS, PACK], BF16, tag="grouped", align_bytes=64)
+            nc.vector.tensor_scalar_max(
+                out=grouped[:].rearrange("p (c i) j -> p c j i", i=RUN),
+                in0=act[:].rearrange("p j (c i) -> p c j i", i=RUN),
+                scalar1=0.0,
+            )
+            return grouped
+
+        def quantise_features(u, g, grouped):
+            nc.vector.quantize_mx(
+                out=a_codes[u][:, g, :].bitcast(FP8X4),
+                scales=a_scales[u][:, g, :],
+                in_=grouped[:].rearrange("p t j -> p (t j)"),
+            )
+
+        def similarity_logits(b, n):
+            lang_u, vis_u = 2 * b + LANG, 2 * b + VIS
+            sim = s_psum.tile([P, TOKENS], F32, tag="sim")
+            toks = slice(n * P, (n + 1) * P)
+            for g in range(PASSES):
+                nc.tensor.matmul_mx(
+                    out=sim[:],
+                    lhsT=a_codes[vis_u][:, g, toks].bitcast(FP8X4),
+                    lhsT_scale=a_scales[vis_u][:, g, toks],
+                    rhs=a_codes[lang_u][:, g, :].bitcast(FP8X4),
+                    rhs_scale=a_scales[lang_u][:, g, :],
+                    start=(g == 0),
+                    stop=(g == PASSES - 1),
+                )
+            probs = prob_pool.tile([P, TOKENS], F32, tag="probs")
+            top = stat_pool.tile([P, 1], F32, tag="top")
+            nc.vector.tensor_scalar(
+                out=probs[:], in0=sim[:], scalar1=sharpness[:], scalar2=None,
+                op0=ALU.mult, op1=ALU.max, accum_out=top[:],
+            )
+            neg_top = stat_pool.tile([P, 1], F32, tag="neg_top")
+            nc.vector.tensor_scalar_mul(out=neg_top[:], in0=top[:], scalar1=-1.0)
+            return probs, neg_top
+
+        def exponentials(probs, neg_top):
+            total = stat_pool.tile([P, 1], F32, tag="total")
+            nc.scalar.activation(
+                out=probs[:], in_=probs[:], func=ACT.Exp, bias=neg_top[:], scale=1.0,
+                accum_out=total[:],
+            )
+            return total
+
+        def store_probabilities(b, n, probs, total):
+            inv_total = stat_pool.tile([P, 1], F32, tag="inv_total")
+            nc.vector.reciprocal(out=inv_total[:], in_=total[:])
+            nc.vector.tensor_scalar_mul(out=probs[:], in0=probs[:], scalar1=inv_total[:])
+            first = b * TOKENS + n * P
+            nc.sync.dma_start(out=out_rows[first : first + P, :], in_=probs[:])
+
+        bias_all = const.tile([P, 2, D], F32)
+        for s in (LANG, VIS):
+            for half in range(HALVES):
+                cols = slice(half * BANK, (half + 1) * BANK)
+                spread = h_psum.tile([P, BANK], F32, tag="acc")
+                nc.tensor.matmul(
+                    out=spread[:], lhsT=ones_bf16[:], rhs=bias_rows[:, s, cols],
+                    start=True, stop=True,
+                )
+                nc.scalar.copy(out=bias_all[:, s, cols], in_=spread[:])
+
+        x_grouped = {}
+        x_quantised = {}
+        for i in range(AHEAD):
+            x_grouped[i] = prepare_tokens(i)
+        lang_grouped = {}
+        for g in range(PASSES):
+            lang_grouped[(g, 0)] = regroup_weights(LANG, g, 0, "vector")
+            lang_grouped[(g, 1)] = regroup_weights(LANG, g, 1, "scalar")
+        for i in range(AHEAD):
+            x_quantised[i] = quantise_tokens(x_grouped[i])
+        for half in range(HALVES):
+            for g in range(PASSES):
+                quantise_weights(LANG, g, half, lang_grouped[(g, half)])
+
+        affine_ps = x_psum.tile([P, P], BF16, tag="xT")
+        nc.tensor.transpose(out=affine_ps[:], in_=affine_rows[:], identity=ident_bf16[:])
+        affine = const.tile([P, 4 * CHUNKS], F32)
+        nc.vector.tensor_copy(out=affine[:], in_=affine_ps[:, 0 : 4 * CHUNKS])
+        sharpness = const.tile([P, 1], F32)
+
+        normalised = {}
+        stats = {}
+        acts = {}
+        rows = {}
+        for t in range(STEPS):
+            ages = [t - TILES_PER_UNIT * (u + 1) for u in range(UNITS)]
+
+            for u in range(VIS, UNITS, 2):
+                n = ages[u] - ROWS_FROM
+                if 0 <= n < TILES_PER_UNIT:
+                    rows[(u, n)] = similarity_logits(u // 2, n)
+            if t < N_TILES:
+                normalised[t], neg_mean = project(t, x_quantised[t][0], x_quantised[t][1])
+                stats[t] = [neg_mean, None]
+            if 1 <= t <= N_TILES:
+                normalise(normalised[t - 1], stats[t - 1][0], stats[t - 1][1])
+            for u in range(VIS, UNITS, 2):
+                n = ages[u] - ROWS_FROM - 1
+                if 0 <= n < TILES_PER_UNIT:
+                    store_probabilities(u // 2, n, rows[(u, n)][0], rows[(u, n)][2])
+            feature_group = None
+            for u in range(UNITS):
+                if ages[u] in (2, 4):
+                    feature_group = (u, ages[u] // 2 - 1, regroup_features(acts[u]))
+            weight_group = None
+            if t < PASSES * HALVES:
+                g, half = divmod(t, HALVES)
+                weight_group = (g, half, regroup_weights(VIS, g, half, ("vector", "scalar")[half]))
+
+            if t + AHEAD < N_TILES:
+                x_grouped[t + AHEAD] = prepare_tokens(t + AHEAD)
+            if t < N_TILES:
+                stats[t][1] = squared_deviations(normalised[t], stats[t][0])
+            for u in range(VIS, UNITS, 2):
+                n = ages[u] - ROWS_FROM
+                if 0 <= n < TILES_PER_UNIT:
+                    rows[(u, n)] = rows[(u, n)] + (exponentials(rows[(u, n)][0], rows[(u, n)][1]),)
+            for u in range(UNITS):
+                if 0 <= ages[u] < TILES_PER_UNIT:
+                    for c in range(ages[u] * CHUNKS_PER_STEP, (ages[u] + 1) * CHUNKS_PER_STEP):
+                        if c % PACK == 0:
+                            act = act_pool.tile([P, PACK, TOKENS], BF16, tag="act")
+                            acts[u] = act
+                        transpose_features(u, c, acts[u])
+            if t == CLAW_STEP:
+                claw_cols = s_psum.tile([P, BANK], F32, tag="sim")
+                pieces = D * D // P // BANK
+                for c in range(pieces):
+                    nc.tensor.matmul(
+                        out=claw_cols[:], lhsT=ones_bf16[:],
+                        rhs=claw_sb[:, c * BANK : (c + 1) * BANK],
+                        start=(c == 0), stop=(c == pieces - 1),
+                    )
+                claw_sum = const.tile([P, 1], F32)
+                nc.vector.reduce_sum(out=claw_sum[:], in_=claw_cols[:], axis=AX.X)
+                nc.vector.tensor_scalar_mul(
+                    out=sharpness[:], in0=claw_sum[:], scalar1=1.0 / (D * D * TEMPERATURE)
+                )
+
+            if t + AHEAD < N_TILES:
+                x_quantised[t + AHEAD] = quantise_tokens(x_grouped[t + AHEAD])
+            if feature_group is not None:
+                quantise_features(feature_group[0], feature_group[1], feature_group[2])
+            if weight_group is not None:
+                quantise_weights(VIS, weight_group[0], weight_group[1], weight_group[2])

@@ -29,10 +29,15 @@ LANG, VIS = 0, 1
 UNITS = 2 * BATCHES
 TILES_PER_UNIT = TOKENS // P
 N_TILES = UNITS * TILES_PER_UNIT
-CHUNKS_PER_STEP = CHUNKS // TILES_PER_UNIT
+GROUP_TILES = 2
+GROUP_TOKENS = GROUP_TILES * P
+N_GROUPS = N_TILES // GROUP_TILES
+GROUPS_PER_UNIT = TILES_PER_UNIT // GROUP_TILES
+CHUNKS_PER_BANK = BANK // GROUP_TOKENS
+BANKS_PER_STEP = 2
 AHEAD = 2
-ROWS_FROM = TILES_PER_UNIT + 1
-STEPS = N_TILES + TILES_PER_UNIT + ROWS_FROM + 1
+ROW_LAG = 2 * GROUP_TILES + 1
+STEPS = N_TILES + ROW_LAG + 1
 CLAW_STEP = 2 * TILES_PER_UNIT
 
 FLOPS = 2 * 2 * BATCHES * TOKENS * D * D + 2 * BATCHES * TOKENS * TOKENS * D
@@ -54,11 +59,11 @@ def tile_clawmatrix_pa_kernel(
         resident = ctx.enter_context(tc.tile_pool(name="resident", bufs=1))
         grouped_pool = ctx.enter_context(tc.tile_pool(name="grouped", bufs=4))
         token_pool = ctx.enter_context(tc.tile_pool(name="tokens", bufs=4))
-        row_pool = ctx.enter_context(tc.tile_pool(name="rows", bufs=2 * TILES_PER_UNIT + 1))
+        row_pool = ctx.enter_context(tc.tile_pool(name="rows", bufs=2 * GROUP_TILES + 2))
         scrap_pool = ctx.enter_context(tc.tile_pool(name="scrap", bufs=1))
-        act_pool = ctx.enter_context(tc.tile_pool(name="act", bufs=2))
-        prob_pool = ctx.enter_context(tc.tile_pool(name="probs", bufs=3))
-        stat_pool = ctx.enter_context(tc.tile_pool(name="stats", bufs=4))
+        act_pool = ctx.enter_context(tc.tile_pool(name="act", bufs=3))
+        prob_pool = ctx.enter_context(tc.tile_pool(name="probs", bufs=6))
+        stat_pool = ctx.enter_context(tc.tile_pool(name="stats", bufs=6))
         x_psum = ctx.enter_context(tc.psum_pool(name="x_psum", bufs=1))
         h_psum = ctx.enter_context(tc.psum_pool(name="h_psum", bufs=4))
         y_psum = ctx.enter_context(tc.psum_pool(name="y_psum", bufs=2))
@@ -83,16 +88,25 @@ def tile_clawmatrix_pa_kernel(
                 out=bias_rows[0:1, s, :], in_=biases[s].rearrange("(o d) -> o d", o=1)
             )
 
+        affine_rows = const.tile([P, P], BF16)
+        nc.vector.memset(affine_rows[:], 0.0)
+        for s in (LANG, VIS):
+            for v, vector in enumerate((gains[s], shifts[s])):
+                first = (2 * s + v) * CHUNKS
+                nc.sync.dma_start(
+                    out=affine_rows[first : first + CHUNKS, :],
+                    in_=vector.rearrange("(c p) -> c p", p=P),
+                )
+
+        x_tiles = []
+
         def load_tokens(u):
             s, b = u % 2, u // 2
-            x_unit = resident.tile([P, TILES_PER_UNIT, D], BF16, name="x_unit%d" % u)
-            nc.sync.dma_start(
-                out=x_unit[:],
-                in_=features[s][b * TOKENS : (b + 1) * TOKENS, :].rearrange(
-                    "(n p) k -> p n k", p=P
-                ),
-            )
-            return x_unit
+            for n in range(TILES_PER_UNIT):
+                first = b * TOKENS + n * P
+                x_tile = resident.tile([P, D], BF16, name="x_tile%d" % len(x_tiles))
+                nc.sync.dma_start(out=x_tile[:], in_=features[s][first : first + P, :])
+                x_tiles.append(x_tile)
 
         def load_weights(s):
             w_rows = resident.tile([P, PASSES, PACK, D], BF16, name="w_rows%d" % s)
@@ -105,23 +119,13 @@ def tile_clawmatrix_pa_kernel(
                 )
             return w_rows
 
-        x_units = [None] * UNITS
         w_rows = [None] * 2
-        x_units[0] = load_tokens(0)
         w_rows[LANG] = load_weights(LANG)
-        affine_rows = const.tile([P, P], BF16)
-        nc.vector.memset(affine_rows[:], 0.0)
-        for s in (LANG, VIS):
-            for v, vector in enumerate((gains[s], shifts[s])):
-                first = (2 * s + v) * CHUNKS
-                nc.sync.dma_start(
-                    out=affine_rows[first : first + CHUNKS, :],
-                    in_=vector.rearrange("(c p) -> c p", p=P),
-                )
-        x_units[1] = load_tokens(1)
+        load_tokens(0)
         w_rows[VIS] = load_weights(VIS)
-        x_units[2] = load_tokens(2)
-        x_units[3] = load_tokens(3)
+        load_tokens(1)
+        load_tokens(2)
+        load_tokens(3)
         claw_sb = resident.tile([P, D * D // P], BF16)
         nc.sync.dma_start(out=claw_sb[:], in_=claw.rearrange("(p r) c -> p (r c)", p=P))
 
@@ -157,8 +161,7 @@ def tile_clawmatrix_pa_kernel(
             )
 
         def prepare_tokens(i):
-            u, n = divmod(i, TILES_PER_UNIT)
-            words = x_units[u][:, n, :].bitcast(F32)
+            words = x_tiles[i][:].bitcast(F32)
             xT = x_psum.tile([P, PACK, P], F32, tag="xT")
             for q in range(PACK):
                 nc.tensor.transpose(
@@ -238,23 +241,29 @@ def tile_clawmatrix_pa_kernel(
                 op0=ALU.add, op1=ALU.mult,
             )
 
-        def transpose_features(u, c, act):
-            s = u % 2
-            yT = y_psum.tile([P, TOKENS], F32, tag="yT")
-            for n in range(TILES_PER_UNIT):
-                nc.tensor.transpose(
-                    out=yT[:, n * P : (n + 1) * P],
-                    in_=normalised[u * TILES_PER_UNIT + n][:, c * P : (c + 1) * P],
-                    identity=ident_f32[:],
+        def transpose_features(q, bank, act):
+            s = (q // GROUPS_PER_UNIT) % 2
+            chunks = range(bank * CHUNKS_PER_BANK, (bank + 1) * CHUNKS_PER_BANK)
+            yT = y_psum.tile([P, CHUNKS_PER_BANK, GROUP_TOKENS], F32, tag="yT")
+            for c in chunks:
+                for r in range(GROUP_TILES):
+                    nc.tensor.transpose(
+                        out=yT[:, c % CHUNKS_PER_BANK, r * P : (r + 1) * P],
+                        in_=normalised[q * GROUP_TILES + r][:, c * P : (c + 1) * P],
+                        identity=ident_f32[:],
+                    )
+            for c in chunks:
+                gain = affine[:, 2 * s * CHUNKS + c : 2 * s * CHUNKS + c + 1]
+                shift = affine[:, (2 * s + 1) * CHUNKS + c : (2 * s + 1) * CHUNKS + c + 1]
+                nc.scalar.activation(
+                    out=act[:, c % PACK, :], in_=yT[:, c % CHUNKS_PER_BANK, :],
+                    func=ACT.Identity, scale=gain, bias=shift,
                 )
-            gain = affine[:, 2 * s * CHUNKS + c : 2 * s * CHUNKS + c + 1]
-            shift = affine[:, (2 * s + 1) * CHUNKS + c : (2 * s + 1) * CHUNKS + c + 1]
-            nc.scalar.activation(
-                out=act[:, c % PACK, :], in_=yT[:], func=ACT.Identity, scale=gain, bias=shift
-            )
 
         def regroup_features(act):
-            grouped = grouped_pool.tile([P, TOKENS, PACK], BF16, tag="grouped", align_bytes=64)
+            grouped = grouped_pool.tile(
+                [P, GROUP_TOKENS, PACK], BF16, tag="grouped", align_bytes=64
+            )
             nc.vector.tensor_scalar_max(
                 out=grouped[:].rearrange("p (c i) j -> p c j i", i=RUN),
                 in0=act[:].rearrange("p j (c i) -> p c j i", i=RUN),
@@ -262,10 +271,13 @@ def tile_clawmatrix_pa_kernel(
             )
             return grouped
 
-        def quantise_features(u, g, grouped):
+        def quantise_features(q, g, grouped):
+            u = q // GROUPS_PER_UNIT
+            first = (q % GROUPS_PER_UNIT) * GROUP_TOKENS
+            toks = slice(first, first + GROUP_TOKENS)
             nc.vector.quantize_mx(
-                out=a_codes[u][:, g, :].bitcast(FP8X4),
-                scales=a_scales[u][:, g, :],
+                out=a_codes[u][:, g, toks].bitcast(FP8X4),
+                scales=a_scales[u][:, g, toks],
                 in_=grouped[:].rearrange("p t j -> p (t j)"),
             )
 
@@ -319,50 +331,58 @@ def tile_clawmatrix_pa_kernel(
                 )
                 nc.scalar.copy(out=bias_all[:, s, cols], in_=spread[:])
 
-        x_grouped = {}
-        x_quantised = {}
-        for i in range(AHEAD):
-            x_grouped[i] = prepare_tokens(i)
-        lang_grouped = {}
-        for g in range(PASSES):
-            lang_grouped[(g, 0)] = regroup_weights(LANG, g, 0, "vector")
-            lang_grouped[(g, 1)] = regroup_weights(LANG, g, 1, "scalar")
-        for i in range(AHEAD):
-            x_quantised[i] = quantise_tokens(x_grouped[i])
-        for half in range(HALVES):
-            for g in range(PASSES):
-                quantise_weights(LANG, g, half, lang_grouped[(g, half)])
-
         affine_ps = x_psum.tile([P, P], BF16, tag="xT")
         nc.tensor.transpose(out=affine_ps[:], in_=affine_rows[:], identity=ident_bf16[:])
         affine = const.tile([P, 4 * CHUNKS], F32)
         nc.vector.tensor_copy(out=affine[:], in_=affine_ps[:, 0 : 4 * CHUNKS])
+
+        x_grouped = {}
+        x_quantised = {}
+        lang_grouped = {}
+        for g in range(PASSES):
+            lang_grouped[(g, 0)] = regroup_weights(LANG, g, 0, "vector")
+            lang_grouped[(g, 1)] = regroup_weights(LANG, g, 1, "scalar")
+            if g > 0:
+                quantise_weights(LANG, g - 1, 1, lang_grouped[(g - 1, 1)])
+            quantise_weights(LANG, g, 0, lang_grouped[(g, 0)])
+        for i in range(AHEAD):
+            x_grouped[i] = prepare_tokens(i)
+        quantise_weights(LANG, PASSES - 1, 1, lang_grouped[(PASSES - 1, 1)])
+        for i in range(AHEAD):
+            x_quantised[i] = quantise_tokens(x_grouped[i])
+
         sharpness = const.tile([P, 1], F32)
 
+        def row_step(b, n):
+            if b == 0:
+                return N_TILES + n
+            return (2 * b + VIS) * TILES_PER_UNIT + n + ROW_LAG
+
+        all_rows = [(b, n) for b in range(BATCHES) for n in range(TILES_PER_UNIT)]
         normalised = {}
         stats = {}
         acts = {}
         rows = {}
         for t in range(STEPS):
-            ages = [t - TILES_PER_UNIT * (u + 1) for u in range(UNITS)]
+            ages = [t - GROUP_TILES * (q + 1) for q in range(N_GROUPS)]
 
-            for u in range(VIS, UNITS, 2):
-                n = ages[u] - ROWS_FROM
-                if 0 <= n < TILES_PER_UNIT:
-                    rows[(u, n)] = similarity_logits(u // 2, n)
+            for b, n in all_rows:
+                if t == row_step(b, n):
+                    rows[(b, n)] = similarity_logits(b, n)
             if t < N_TILES:
                 normalised[t], neg_mean = project(t, x_quantised[t][0], x_quantised[t][1])
                 stats[t] = [neg_mean, None]
             if 1 <= t <= N_TILES:
                 normalise(normalised[t - 1], stats[t - 1][0], stats[t - 1][1])
-            for u in range(VIS, UNITS, 2):
-                n = ages[u] - ROWS_FROM - 1
-                if 0 <= n < TILES_PER_UNIT:
-                    store_probabilities(u // 2, n, rows[(u, n)][0], rows[(u, n)][2])
-            feature_group = None
-            for u in range(UNITS):
-                if ages[u] in (2, 4):
-                    feature_group = (u, ages[u] // 2 - 1, regroup_features(acts[u]))
+            for b, n in all_rows:
+                if t == row_step(b, n) + 1:
+                    store_probabilities(b, n, rows[(b, n)][0], rows[(b, n)][2])
+            feature_groups = []
+            for q in range(N_GROUPS):
+                for g in range(PASSES):
+                    last_bank = ((g + 1) * PACK - 1) // CHUNKS_PER_BANK
+                    if ages[q] == last_bank // BANKS_PER_STEP + 1:
+                        feature_groups.append((q, g, regroup_features(acts[(q, g)])))
             weight_group = None
             if t < PASSES * HALVES:
                 g, half = divmod(t, HALVES)
@@ -372,17 +392,17 @@ def tile_clawmatrix_pa_kernel(
                 x_grouped[t + AHEAD] = prepare_tokens(t + AHEAD)
             if t < N_TILES:
                 stats[t][1] = squared_deviations(normalised[t], stats[t][0])
-            for u in range(VIS, UNITS, 2):
-                n = ages[u] - ROWS_FROM
-                if 0 <= n < TILES_PER_UNIT:
-                    rows[(u, n)] = rows[(u, n)] + (exponentials(rows[(u, n)][0], rows[(u, n)][1]),)
-            for u in range(UNITS):
-                if 0 <= ages[u] < TILES_PER_UNIT:
-                    for c in range(ages[u] * CHUNKS_PER_STEP, (ages[u] + 1) * CHUNKS_PER_STEP):
-                        if c % PACK == 0:
-                            act = act_pool.tile([P, PACK, TOKENS], BF16, tag="act")
-                            acts[u] = act
-                        transpose_features(u, c, acts[u])
+            for b, n in all_rows:
+                if t == row_step(b, n):
+                    rows[(b, n)] = rows[(b, n)] + (exponentials(rows[(b, n)][0], rows[(b, n)][1]),)
+            for q in range(N_GROUPS):
+                if 0 <= ages[q] < GROUP_TILES:
+                    for bank in range(ages[q] * BANKS_PER_STEP, (ages[q] + 1) * BANKS_PER_STEP):
+                        g = bank * CHUNKS_PER_BANK // PACK
+                        if (q, g) not in acts:
+                            act = act_pool.tile([P, PACK, GROUP_TOKENS], BF16, tag="act")
+                            acts[(q, g)] = act
+                        transpose_features(q, bank, acts[(q, g)])
             if t == CLAW_STEP:
                 claw_cols = s_psum.tile([P, BANK], F32, tag="sim")
                 pieces = D * D // P // BANK
@@ -400,7 +420,7 @@ def tile_clawmatrix_pa_kernel(
 
             if t + AHEAD < N_TILES:
                 x_quantised[t + AHEAD] = quantise_tokens(x_grouped[t + AHEAD])
-            if feature_group is not None:
-                quantise_features(feature_group[0], feature_group[1], feature_group[2])
+            for q, g, grouped in feature_groups:
+                quantise_features(q, g, grouped)
             if weight_group is not None:
                 quantise_weights(VIS, weight_group[0], weight_group[1], weight_group[2])

@@ -35,7 +35,7 @@ N_GROUPS = N_TILES // GROUP_TILES
 GROUPS_PER_UNIT = TILES_PER_UNIT // GROUP_TILES
 CHUNKS_PER_BANK = BANK // GROUP_TOKENS
 BANKS_PER_STEP = 2
-AHEAD = 2
+AHEAD = 3
 ROW_LAG = 2 * GROUP_TILES + 1
 STEPS = N_TILES + ROW_LAG + 1
 CLAW_STEP = 2 * TILES_PER_UNIT
@@ -58,7 +58,7 @@ def tile_clawmatrix_pa_kernel(
         const = ctx.enter_context(tc.tile_pool(name="const", bufs=1))
         resident = ctx.enter_context(tc.tile_pool(name="resident", bufs=1))
         grouped_pool = ctx.enter_context(tc.tile_pool(name="grouped", bufs=4))
-        token_pool = ctx.enter_context(tc.tile_pool(name="tokens", bufs=4))
+        token_pool = ctx.enter_context(tc.tile_pool(name="tokens", bufs=AHEAD + 2))
         row_pool = ctx.enter_context(tc.tile_pool(name="rows", bufs=2 * GROUP_TILES + 2))
         scrap_pool = ctx.enter_context(tc.tile_pool(name="scrap", bufs=1))
         act_pool = ctx.enter_context(tc.tile_pool(name="act", bufs=3))
@@ -68,35 +68,35 @@ def tile_clawmatrix_pa_kernel(
         h_psum = ctx.enter_context(tc.psum_pool(name="h_psum", bufs=4))
         y_psum = ctx.enter_context(tc.psum_pool(name="y_psum", bufs=2))
         s_psum = ctx.enter_context(tc.psum_pool(name="s_psum", bufs=1))
+        ctx.enter_context(tc.manual_schedule())
 
-        ident_f32 = const.tile([P, P], F32)
-        make_identity(nc, ident_f32[:])
-        ident_bf16 = const.tile([P, P], BF16)
-        nc.vector.tensor_copy(out=ident_bf16[:], in_=ident_f32[:])
+        bias_rows = const.tile([P, 2, D], BF16)
+        nc.vector.memset(bias_rows[:], 0.0)
+        affine_rows = const.tile([P, P], BF16)
+        nc.vector.memset(affine_rows[:], 0.0)
+        for s in (LANG, VIS):
+            nc.scalar.dma_start(
+                out=bias_rows[0:1, s, :], in_=biases[s].rearrange("(o d) -> o d", o=1)
+            )
+        for s in (LANG, VIS):
+            for v, vector in enumerate((gains[s], shifts[s])):
+                first = (2 * s + v) * CHUNKS
+                nc.scalar.dma_start(
+                    out=affine_rows[first : first + CHUNKS, :],
+                    in_=vector.rearrange("(c p) -> c p", p=P),
+                )
+
+        warm = const.tile([P, 1], F32)
+        nc.vector.memset(warm[:], 0.0)
+        nc.scalar.activation(out=warm[:], in_=warm[:], func=ACT.Exp)
         ones_bf16 = const.tile([P, P], BF16)
         nc.vector.memset(ones_bf16[:], 1.0)
         minus_half = const.tile([P, 1], F32)
         nc.vector.memset(minus_half[:], -0.5)
-        warm = const.tile([P, 1], F32)
-        nc.vector.memset(warm[:], 0.0)
-        nc.scalar.activation(out=warm[:], in_=warm[:], func=ACT.Exp)
-
-        bias_rows = const.tile([P, 2, D], BF16)
-        nc.vector.memset(bias_rows[:], 0.0)
-        for s in (LANG, VIS):
-            nc.sync.dma_start(
-                out=bias_rows[0:1, s, :], in_=biases[s].rearrange("(o d) -> o d", o=1)
-            )
-
-        affine_rows = const.tile([P, P], BF16)
-        nc.vector.memset(affine_rows[:], 0.0)
-        for s in (LANG, VIS):
-            for v, vector in enumerate((gains[s], shifts[s])):
-                first = (2 * s + v) * CHUNKS
-                nc.sync.dma_start(
-                    out=affine_rows[first : first + CHUNKS, :],
-                    in_=vector.rearrange("(c p) -> c p", p=P),
-                )
+        ident_f32 = const.tile([P, P], F32)
+        make_identity(nc, ident_f32[:])
+        ident_bf16 = const.tile([P, P], BF16)
+        nc.vector.tensor_copy(out=ident_bf16[:], in_=ident_f32[:])
 
         x_tiles = []
 
@@ -109,15 +109,15 @@ def tile_clawmatrix_pa_kernel(
                 x_tiles.append(x_tile)
 
         def load_weights(s):
-            w_rows = resident.tile([P, PASSES, PACK, D], BF16, name="w_rows%d" % s)
+            rows_of_s = resident.tile([P, PASSES, PACK, D], BF16, name="w_rows%d" % s)
             for g in range(PASSES):
                 nc.sync.dma_start(
-                    out=w_rows[:, g, :, :].rearrange("q (u e) d -> q u e d", u=2),
+                    out=rows_of_s[:, g, :, :].rearrange("q (u e) d -> q u e d", u=2),
                     in_=weights[s][g * K_PASS : (g + 1) * K_PASS, :].rearrange(
                         "(u q e) d -> q u e d", u=2, e=2
                     ),
                 )
-            return w_rows
+            return rows_of_s
 
         w_rows = [None] * 2
         w_rows[LANG] = load_weights(LANG)
@@ -183,8 +183,7 @@ def tile_clawmatrix_pa_kernel(
 
         def project(i, x_codes, x_scales):
             s = (i // TILES_PER_UNIT) % 2
-            h = row_pool.tile([P, D], F32, tag="h")
-            sums = stat_pool.tile([P, HALVES], F32, tag="sums")
+            banks = []
             for half in range(HALVES):
                 cols = slice(half * BANK, (half + 1) * BANK)
                 acc = h_psum.tile([P, BANK], F32, tag="acc")
@@ -199,9 +198,18 @@ def tile_clawmatrix_pa_kernel(
                         start=(g == 0),
                         stop=(g == PASSES - 1),
                     )
+                banks.append(acc)
+            return banks
+
+        def add_bias(i, banks):
+            s = (i // TILES_PER_UNIT) % 2
+            h = row_pool.tile([P, D], F32, tag="h")
+            sums = stat_pool.tile([P, HALVES], F32, tag="sums")
+            for half in range(HALVES):
+                cols = slice(half * BANK, (half + 1) * BANK)
                 nc.vector.scalar_tensor_tensor(
                     out=h[:, cols],
-                    in0=acc[:],
+                    in0=banks[half][:],
                     scalar=1.0,
                     in1=bias_all[:, s, cols],
                     op0=ALU.mult,
@@ -296,19 +304,17 @@ def tile_clawmatrix_pa_kernel(
                     stop=(g == PASSES - 1),
                 )
             probs = prob_pool.tile([P, TOKENS], F32, tag="probs")
-            top = stat_pool.tile([P, 1], F32, tag="top")
-            nc.vector.tensor_scalar(
-                out=probs[:], in0=sim[:], scalar1=sharpness[:], scalar2=None,
-                op0=ALU.mult, op1=ALU.max, accum_out=top[:],
-            )
             neg_top = stat_pool.tile([P, 1], F32, tag="neg_top")
-            nc.vector.tensor_scalar_mul(out=neg_top[:], in0=top[:], scalar1=-1.0)
+            nc.vector.tensor_scalar(
+                out=probs[:], in0=sim[:], scalar1=neg_sharpness[:], scalar2=None,
+                op0=ALU.mult, op1=ALU.min, accum_out=neg_top[:],
+            )
             return probs, neg_top
 
         def exponentials(probs, neg_top):
             total = stat_pool.tile([P, 1], F32, tag="total")
             nc.scalar.activation(
-                out=probs[:], in_=probs[:], func=ACT.Exp, bias=neg_top[:], scale=1.0,
+                out=probs[:], in_=probs[:], func=ACT.Exp, bias=neg_top[:], scale=-1.0,
                 accum_out=total[:],
             )
             return total
@@ -316,7 +322,10 @@ def tile_clawmatrix_pa_kernel(
         def store_probabilities(b, n, probs, total):
             inv_total = stat_pool.tile([P, 1], F32, tag="inv_total")
             nc.vector.reciprocal(out=inv_total[:], in_=total[:])
-            nc.vector.tensor_scalar_mul(out=probs[:], in0=probs[:], scalar1=inv_total[:])
+            nc.gpsimd.tensor_scalar(
+                out=probs[:], in0=probs[:], scalar1=inv_total[:], scalar2=0.0,
+                op0=ALU.mult, op1=ALU.add,
+            )
             first = b * TOKENS + n * P
             nc.sync.dma_start(out=out_rows[first : first + P, :], in_=probs[:])
 
@@ -351,7 +360,7 @@ def tile_clawmatrix_pa_kernel(
         for i in range(AHEAD):
             x_quantised[i] = quantise_tokens(x_grouped[i])
 
-        sharpness = const.tile([P, 1], F32)
+        neg_sharpness = const.tile([P, 1], F32)
 
         def row_step(b, n):
             if b == 0:
@@ -359,6 +368,7 @@ def tile_clawmatrix_pa_kernel(
             return (2 * b + VIS) * TILES_PER_UNIT + n + ROW_LAG
 
         all_rows = [(b, n) for b in range(BATCHES) for n in range(TILES_PER_UNIT)]
+        projected = {0: project(0, x_quantised[0][0], x_quantised[0][1])}
         normalised = {}
         stats = {}
         acts = {}
@@ -369,8 +379,10 @@ def tile_clawmatrix_pa_kernel(
             for b, n in all_rows:
                 if t == row_step(b, n):
                     rows[(b, n)] = similarity_logits(b, n)
+            if t + 1 < N_TILES:
+                projected[t + 1] = project(t + 1, x_quantised[t + 1][0], x_quantised[t + 1][1])
             if t < N_TILES:
-                normalised[t], neg_mean = project(t, x_quantised[t][0], x_quantised[t][1])
+                normalised[t], neg_mean = add_bias(t, projected[t])
                 stats[t] = [neg_mean, None]
             if 1 <= t <= N_TILES:
                 normalise(normalised[t - 1], stats[t - 1][0], stats[t - 1][1])
@@ -383,10 +395,10 @@ def tile_clawmatrix_pa_kernel(
                     last_bank = ((g + 1) * PACK - 1) // CHUNKS_PER_BANK
                     if ages[q] == last_bank // BANKS_PER_STEP + 1:
                         feature_groups.append((q, g, regroup_features(acts[(q, g)])))
-            weight_group = None
-            if t < PASSES * HALVES:
-                g, half = divmod(t, HALVES)
-                weight_group = (g, half, regroup_weights(VIS, g, half, ("vector", "scalar")[half]))
+            weight_groups = []
+            if t < PASSES:
+                weight_groups.append((t, 0, regroup_weights(VIS, t, 0, "vector")))
+                weight_groups.append((t, 1, regroup_weights(VIS, t, 1, "scalar")))
 
             if t + AHEAD < N_TILES:
                 x_grouped[t + AHEAD] = prepare_tokens(t + AHEAD)
@@ -415,12 +427,12 @@ def tile_clawmatrix_pa_kernel(
                 claw_sum = const.tile([P, 1], F32)
                 nc.vector.reduce_sum(out=claw_sum[:], in_=claw_cols[:], axis=AX.X)
                 nc.vector.tensor_scalar_mul(
-                    out=sharpness[:], in0=claw_sum[:], scalar1=1.0 / (D * D * TEMPERATURE)
+                    out=neg_sharpness[:], in0=claw_sum[:], scalar1=-1.0 / (D * D * TEMPERATURE)
                 )
 
             if t + AHEAD < N_TILES:
                 x_quantised[t + AHEAD] = quantise_tokens(x_grouped[t + AHEAD])
             for q, g, grouped in feature_groups:
                 quantise_features(q, g, grouped)
-            if weight_group is not None:
-                quantise_weights(VIS, weight_group[0], weight_group[1], weight_group[2])
+            for g, half, grouped in weight_groups:
+                quantise_weights(VIS, g, half, grouped)

@@ -35,10 +35,11 @@ N_GROUPS = N_TILES // GROUP_TILES
 GROUPS_PER_UNIT = TILES_PER_UNIT // GROUP_TILES
 CHUNKS_PER_BANK = BANK // GROUP_TOKENS
 BANKS_PER_STEP = 2
-AHEAD = 3
-ROW_LAG = 2 * GROUP_TILES + 1
+AHEAD = 2
+ROW_LAG = 2 * GROUP_TILES + 3
 STEPS = N_TILES + ROW_LAG + 1
-CLAW_STEP = 2 * TILES_PER_UNIT
+CLAW_PIECES = D * D // P // BANK
+CLAW_STEP = 6
 
 FLOPS = 2 * 2 * BATCHES * TOKENS * D * D + 2 * BATCHES * TOKENS * TOKENS * D
 
@@ -59,44 +60,34 @@ def tile_clawmatrix_pa_kernel(
         resident = ctx.enter_context(tc.tile_pool(name="resident", bufs=1))
         grouped_pool = ctx.enter_context(tc.tile_pool(name="grouped", bufs=4))
         token_pool = ctx.enter_context(tc.tile_pool(name="tokens", bufs=AHEAD + 2))
-        row_pool = ctx.enter_context(tc.tile_pool(name="rows", bufs=2 * GROUP_TILES + 2))
+        row_pool = ctx.enter_context(tc.tile_pool(name="rows", bufs=2 * GROUP_TILES + 3))
         scrap_pool = ctx.enter_context(tc.tile_pool(name="scrap", bufs=1))
         act_pool = ctx.enter_context(tc.tile_pool(name="act", bufs=3))
-        prob_pool = ctx.enter_context(tc.tile_pool(name="probs", bufs=6))
+        prob_pool = ctx.enter_context(tc.tile_pool(name="probs", bufs=BATCHES * TILES_PER_UNIT))
         stat_pool = ctx.enter_context(tc.tile_pool(name="stats", bufs=6))
         x_psum = ctx.enter_context(tc.psum_pool(name="x_psum", bufs=1))
-        h_psum = ctx.enter_context(tc.psum_pool(name="h_psum", bufs=4))
-        y_psum = ctx.enter_context(tc.psum_pool(name="y_psum", bufs=2))
-        s_psum = ctx.enter_context(tc.psum_pool(name="s_psum", bufs=1))
+        h_psum = ctx.enter_context(tc.psum_pool(name="h_psum", bufs=HALVES))
+        y_psum = ctx.enter_context(tc.psum_pool(name="y_psum", bufs=4))
+        c_psum = ctx.enter_context(tc.psum_pool(name="c_psum", bufs=1))
         ctx.enter_context(tc.manual_schedule())
 
         bias_rows = const.tile([P, 2, D], BF16)
         nc.vector.memset(bias_rows[:], 0.0)
-        affine_rows = const.tile([P, P], BF16)
-        nc.vector.memset(affine_rows[:], 0.0)
         for s in (LANG, VIS):
-            nc.scalar.dma_start(
+            nc.sync.dma_start(
                 out=bias_rows[0:1, s, :], in_=biases[s].rearrange("(o d) -> o d", o=1)
             )
-        for s in (LANG, VIS):
-            for v, vector in enumerate((gains[s], shifts[s])):
-                first = (2 * s + v) * CHUNKS
-                nc.scalar.dma_start(
-                    out=affine_rows[first : first + CHUNKS, :],
-                    in_=vector.rearrange("(c p) -> c p", p=P),
-                )
+        affine_rows = const.tile([P, P], BF16)
+        nc.vector.memset(affine_rows[:], 0.0)
 
-        warm = const.tile([P, 1], F32)
-        nc.vector.memset(warm[:], 0.0)
-        nc.scalar.activation(out=warm[:], in_=warm[:], func=ACT.Exp)
-        ones_bf16 = const.tile([P, P], BF16)
-        nc.vector.memset(ones_bf16[:], 1.0)
-        minus_half = const.tile([P, 1], F32)
-        nc.vector.memset(minus_half[:], -0.5)
-        ident_f32 = const.tile([P, P], F32)
-        make_identity(nc, ident_f32[:])
-        ident_bf16 = const.tile([P, P], BF16)
-        nc.vector.tensor_copy(out=ident_bf16[:], in_=ident_f32[:])
+        def load_gains_and_shifts():
+            for s in (LANG, VIS):
+                for v, vector in enumerate((gains[s], shifts[s])):
+                    first = (2 * s + v) * CHUNKS
+                    nc.sync.dma_start(
+                        out=affine_rows[first : first + CHUNKS, :],
+                        in_=vector.rearrange("(c p) -> c p", p=P),
+                    )
 
         x_tiles = []
 
@@ -122,12 +113,25 @@ def tile_clawmatrix_pa_kernel(
         w_rows = [None] * 2
         w_rows[LANG] = load_weights(LANG)
         load_tokens(0)
+        load_gains_and_shifts()
         w_rows[VIS] = load_weights(VIS)
         load_tokens(1)
         load_tokens(2)
         load_tokens(3)
         claw_sb = resident.tile([P, D * D // P], BF16)
         nc.sync.dma_start(out=claw_sb[:], in_=claw.rearrange("(p r) c -> p (r c)", p=P))
+
+        warm = const.tile([P, 1], F32)
+        nc.vector.memset(warm[:], 0.0)
+        nc.scalar.activation(out=warm[:], in_=warm[:], func=ACT.Exp)
+        minus_half = const.tile([P, 1], F32)
+        nc.vector.memset(minus_half[:], -0.5)
+        ones_bf16 = const.tile([P, P], BF16)
+        nc.vector.memset(ones_bf16[:], 1.0)
+        ident_f32 = const.tile([P, P], F32)
+        make_identity(nc, ident_f32[:])
+        ident_bf16 = const.tile([P, P], BF16)
+        nc.vector.tensor_copy(out=ident_bf16[:], in_=ident_f32[:])
 
         w_codes, w_scales, a_codes, a_scales = [], [], [], []
         for s in (LANG, VIS):
@@ -160,13 +164,16 @@ def tile_clawmatrix_pa_kernel(
                 in_=grouped[:].rearrange("p d t -> p (d t)"),
             )
 
-        def prepare_tokens(i):
+        def transpose_tokens(i):
             words = x_tiles[i][:].bitcast(F32)
             xT = x_psum.tile([P, PACK, P], F32, tag="xT")
             for q in range(PACK):
                 nc.tensor.transpose(
                     out=xT[:, q, :], in_=words[:, q * P : (q + 1) * P], identity=ident_f32[:]
                 )
+            return xT
+
+        def regroup_tokens(xT):
             x_grouped = token_pool.tile([P, PASSES, P, 2], F32, tag="x_grouped", align_bytes=64)
             nc.scalar.copy(out=x_grouped[:], in_=xT[:].rearrange("p (g u) t -> p g t u", u=2))
             return x_grouped
@@ -181,41 +188,38 @@ def tile_clawmatrix_pa_kernel(
             )
             return x_codes, x_scales
 
-        def project(i, x_codes, x_scales):
+        def project(i, half):
             s = (i // TILES_PER_UNIT) % 2
-            banks = []
-            for half in range(HALVES):
-                cols = slice(half * BANK, (half + 1) * BANK)
-                acc = h_psum.tile([P, BANK], F32, tag="acc")
-                for g in range(PASSES):
-                    toks = slice(g * P, (g + 1) * P)
-                    nc.tensor.matmul_mx(
-                        out=acc[:],
-                        lhsT=x_codes[:, toks].bitcast(FP8X4),
-                        lhsT_scale=x_scales[:, toks],
-                        rhs=w_codes[s][:, g, cols].bitcast(FP8X4),
-                        rhs_scale=w_scales[s][:, g, cols],
-                        start=(g == 0),
-                        stop=(g == PASSES - 1),
-                    )
-                banks.append(acc)
-            return banks
-
-        def add_bias(i, banks):
-            s = (i // TILES_PER_UNIT) % 2
-            h = row_pool.tile([P, D], F32, tag="h")
-            sums = stat_pool.tile([P, HALVES], F32, tag="sums")
-            for half in range(HALVES):
-                cols = slice(half * BANK, (half + 1) * BANK)
-                nc.vector.scalar_tensor_tensor(
-                    out=h[:, cols],
-                    in0=banks[half][:],
-                    scalar=1.0,
-                    in1=bias_all[:, s, cols],
-                    op0=ALU.mult,
-                    op1=ALU.add,
-                    accum_out=sums[:, half : half + 1],
+            x_codes, x_scales = x_quantised[i]
+            cols = slice(half * BANK, (half + 1) * BANK)
+            acc = h_psum.tile([P, BANK], F32, tag="acc")
+            for g in range(PASSES):
+                toks = slice(g * P, (g + 1) * P)
+                nc.tensor.matmul_mx(
+                    out=acc[:],
+                    lhsT=x_codes[:, toks].bitcast(FP8X4),
+                    lhsT_scale=x_scales[:, toks],
+                    rhs=w_codes[s][:, g, cols].bitcast(FP8X4),
+                    rhs_scale=w_scales[s][:, g, cols],
+                    start=(g == 0),
+                    stop=(g == PASSES - 1),
                 )
+            return acc
+
+        def add_bias(i, half, acc, h, sums):
+            s = (i // TILES_PER_UNIT) % 2
+            cols = slice(half * BANK, (half + 1) * BANK)
+            nc.vector.scalar_tensor_tensor(
+                out=h[:, cols],
+                in0=acc[:],
+                scalar=1.0,
+                in1=bias_all[:, s, cols],
+                op0=ALU.mult,
+                op1=ALU.add,
+                accum_out=sums[:, half : half + 1],
+            )
+
+        def minus_mean(sums):
             neg_mean = stat_pool.tile([P, 1], F32, tag="neg_mean")
             nc.vector.tensor_scalar(
                 out=neg_mean[:],
@@ -225,7 +229,7 @@ def tile_clawmatrix_pa_kernel(
                 op0=ALU.add,
                 op1=ALU.mult,
             )
-            return h, neg_mean
+            return neg_mean
 
         def squared_deviations(h, neg_mean):
             scrap = scrap_pool.tile([P, D], BF16, tag="scrap")
@@ -236,7 +240,7 @@ def tile_clawmatrix_pa_kernel(
             )
             return ssq
 
-        def normalise(h, neg_mean, ssq):
+        def inverse_deviation(ssq):
             var_eps = stat_pool.tile([P, 1], F32, tag="var_eps")
             nc.gpsimd.tensor_scalar(
                 out=var_eps[:], in0=ssq[:], scalar1=1.0 / D, scalar2=EPS,
@@ -244,23 +248,28 @@ def tile_clawmatrix_pa_kernel(
             )
             rstd = stat_pool.tile([P, 1], F32, tag="rstd")
             nc.gpsimd.tensor_tensor(out=rstd[:], in0=var_eps[:], in1=minus_half[:], op=ALU.pow)
+            return rstd
+
+        def normalise(h, neg_mean, rstd):
             nc.vector.tensor_scalar(
                 out=h[:], in0=h[:], scalar1=neg_mean[:], scalar2=rstd[:],
                 op0=ALU.add, op1=ALU.mult,
             )
 
-        def transpose_features(q, bank, act):
-            s = (q // GROUPS_PER_UNIT) % 2
-            chunks = range(bank * CHUNKS_PER_BANK, (bank + 1) * CHUNKS_PER_BANK)
+        def transpose_features(q, bank):
             yT = y_psum.tile([P, CHUNKS_PER_BANK, GROUP_TOKENS], F32, tag="yT")
-            for c in chunks:
+            for c in range(bank * CHUNKS_PER_BANK, (bank + 1) * CHUNKS_PER_BANK):
                 for r in range(GROUP_TILES):
                     nc.tensor.transpose(
                         out=yT[:, c % CHUNKS_PER_BANK, r * P : (r + 1) * P],
                         in_=normalised[q * GROUP_TILES + r][:, c * P : (c + 1) * P],
                         identity=ident_f32[:],
                     )
-            for c in chunks:
+            return yT
+
+        def gain_and_shift(q, bank, yT, act):
+            s = (q // GROUPS_PER_UNIT) % 2
+            for c in range(bank * CHUNKS_PER_BANK, (bank + 1) * CHUNKS_PER_BANK):
                 gain = affine[:, 2 * s * CHUNKS + c : 2 * s * CHUNKS + c + 1]
                 shift = affine[:, (2 * s + 1) * CHUNKS + c : (2 * s + 1) * CHUNKS + c + 1]
                 nc.scalar.activation(
@@ -289,9 +298,9 @@ def tile_clawmatrix_pa_kernel(
                 in_=grouped[:].rearrange("p t j -> p (t j)"),
             )
 
-        def similarity_logits(b, n):
+        def similarity(b, n):
             lang_u, vis_u = 2 * b + LANG, 2 * b + VIS
-            sim = s_psum.tile([P, TOKENS], F32, tag="sim")
+            sim = h_psum.tile([P, TOKENS], F32, tag="acc")
             toks = slice(n * P, (n + 1) * P)
             for g in range(PASSES):
                 nc.tensor.matmul_mx(
@@ -303,6 +312,9 @@ def tile_clawmatrix_pa_kernel(
                     start=(g == 0),
                     stop=(g == PASSES - 1),
                 )
+            return sim
+
+        def negated_logits(sim):
             probs = prob_pool.tile([P, TOKENS], F32, tag="probs")
             neg_top = stat_pool.tile([P, 1], F32, tag="neg_top")
             nc.vector.tensor_scalar(
@@ -340,11 +352,6 @@ def tile_clawmatrix_pa_kernel(
                 )
                 nc.scalar.copy(out=bias_all[:, s, cols], in_=spread[:])
 
-        affine_ps = x_psum.tile([P, P], BF16, tag="xT")
-        nc.tensor.transpose(out=affine_ps[:], in_=affine_rows[:], identity=ident_bf16[:])
-        affine = const.tile([P, 4 * CHUNKS], F32)
-        nc.vector.tensor_copy(out=affine[:], in_=affine_ps[:, 0 : 4 * CHUNKS])
-
         x_grouped = {}
         x_quantised = {}
         lang_grouped = {}
@@ -355,12 +362,20 @@ def tile_clawmatrix_pa_kernel(
                 quantise_weights(LANG, g - 1, 1, lang_grouped[(g - 1, 1)])
             quantise_weights(LANG, g, 0, lang_grouped[(g, 0)])
         for i in range(AHEAD):
-            x_grouped[i] = prepare_tokens(i)
+            x_grouped[i] = regroup_tokens(transpose_tokens(i))
         quantise_weights(LANG, PASSES - 1, 1, lang_grouped[(PASSES - 1, 1)])
         for i in range(AHEAD):
             x_quantised[i] = quantise_tokens(x_grouped[i])
 
         neg_sharpness = const.tile([P, 1], F32)
+        claw_cols = c_psum.tile([P, BANK], F32)
+
+        def add_claw_block(piece):
+            nc.tensor.matmul(
+                out=claw_cols[:], lhsT=ones_bf16[:],
+                rhs=claw_sb[:, piece * BANK : (piece + 1) * BANK],
+                start=(piece == 0), stop=(piece == CLAW_PIECES - 1),
+            )
 
         def row_step(b, n):
             if b == 0:
@@ -368,71 +383,94 @@ def tile_clawmatrix_pa_kernel(
             return (2 * b + VIS) * TILES_PER_UNIT + n + ROW_LAG
 
         all_rows = [(b, n) for b in range(BATCHES) for n in range(TILES_PER_UNIT)]
-        projected = {0: project(0, x_quantised[0][0], x_quantised[0][1])}
+        projected = {0: [project(0, half) for half in range(HALVES)]}
+        affine_ps = x_psum.tile([P, P], BF16, tag="xT")
+        nc.tensor.transpose(out=affine_ps[:], in_=affine_rows[:], identity=ident_bf16[:])
+        affine = const.tile([P, 4 * CHUNKS], F32)
+        nc.vector.tensor_copy(out=affine[:], in_=affine_ps[:, 0 : 4 * CHUNKS])
         normalised = {}
-        stats = {}
+        neg_means = {}
+        ssqs = {}
         acts = {}
-        rows = {}
+        probs = {}
+        neg_tops = {}
+        totals = {}
+        scalar_weight_groups = []
         for t in range(STEPS):
-            ages = [t - GROUP_TILES * (q + 1) for q in range(N_GROUPS)]
+            ages = [t - GROUP_TILES * (q + 1) - 2 for q in range(N_GROUPS)]
+            rows_now = [row for row in all_rows if row_step(row[0], row[1]) == t]
+            rows_before = [row for row in all_rows if row_step(row[0], row[1]) == t - 1]
+            transposing = [q for q in range(N_GROUPS) if 0 <= ages[q] < GROUP_TILES]
+            claw_piece = 2 * (t - CLAW_STEP)
 
-            for b, n in all_rows:
-                if t == row_step(b, n):
-                    rows[(b, n)] = similarity_logits(b, n)
-            if t + 1 < N_TILES:
-                projected[t + 1] = project(t + 1, x_quantised[t + 1][0], x_quantised[t + 1][1])
+            sims = [similarity(b, n) for b, n in rows_now]
+            banks = {}
+            xT = None
+            for half in range(HALVES):
+                if t + 1 < N_TILES:
+                    if half == 0:
+                        projected[t + 1] = []
+                    projected[t + 1].append(project(t + 1, half))
+                if 0 <= claw_piece < CLAW_PIECES:
+                    add_claw_block(claw_piece + half)
+                for q in transposing:
+                    bank = ages[q] * BANKS_PER_STEP + half
+                    banks[(q, bank)] = transpose_features(q, bank)
+                if half == 0 and t + AHEAD < N_TILES:
+                    xT = transpose_tokens(t + AHEAD)
+
+            for row, sim in zip(rows_now, sims):
+                probs[row], neg_tops[row] = negated_logits(sim)
             if t < N_TILES:
-                normalised[t], neg_mean = add_bias(t, projected[t])
-                stats[t] = [neg_mean, None]
-            if 1 <= t <= N_TILES:
-                normalise(normalised[t - 1], stats[t - 1][0], stats[t - 1][1])
-            for b, n in all_rows:
-                if t == row_step(b, n) + 1:
-                    store_probabilities(b, n, rows[(b, n)][0], rows[(b, n)][2])
+                h = row_pool.tile([P, D], F32, tag="h")
+                sums = stat_pool.tile([P, HALVES], F32, tag="sums")
+                normalised[t] = h
+                add_bias(t, 0, projected[t][0], h, sums)
             feature_groups = []
             for q in range(N_GROUPS):
                 for g in range(PASSES):
                     last_bank = ((g + 1) * PACK - 1) // CHUNKS_PER_BANK
                     if ages[q] == last_bank // BANKS_PER_STEP + 1:
                         feature_groups.append((q, g, regroup_features(acts[(q, g)])))
-            weight_groups = []
+            if 2 <= t <= N_TILES + 1:
+                rstd = inverse_deviation(ssqs[t - 2])
+                normalise(normalised[t - 2], neg_means[t - 2], rstd)
+            for b, n in rows_before:
+                store_probabilities(b, n, probs[(b, n)], totals[(b, n)])
+
+            if xT is not None:
+                x_grouped[t + AHEAD] = regroup_tokens(xT)
+            for q, bank in sorted(banks):
+                g = bank * CHUNKS_PER_BANK // PACK
+                if (q, g) not in acts:
+                    act = act_pool.tile([P, PACK, GROUP_TOKENS], BF16, tag="act")
+                    acts[(q, g)] = act
+                gain_and_shift(q, bank, banks[(q, bank)], acts[(q, g)])
+
+            if t < N_TILES:
+                add_bias(t, 1, projected[t][1], normalised[t], sums)
+                neg_means[t] = minus_mean(sums)
+
+            if t < N_TILES:
+                ssqs[t] = squared_deviations(normalised[t], neg_means[t])
+            for row in rows_now:
+                totals[row] = exponentials(probs[row], neg_tops[row])
+            weight_groups = scalar_weight_groups
+            scalar_weight_groups = []
+            if t < PASSES:
+                scalar_weight_groups.append((t, 1, regroup_weights(VIS, t, 1, "scalar")))
+
             if t < PASSES:
                 weight_groups.append((t, 0, regroup_weights(VIS, t, 0, "vector")))
-                weight_groups.append((t, 1, regroup_weights(VIS, t, 1, "scalar")))
-
-            if t + AHEAD < N_TILES:
-                x_grouped[t + AHEAD] = prepare_tokens(t + AHEAD)
-            if t < N_TILES:
-                stats[t][1] = squared_deviations(normalised[t], stats[t][0])
-            for b, n in all_rows:
-                if t == row_step(b, n):
-                    rows[(b, n)] = rows[(b, n)] + (exponentials(rows[(b, n)][0], rows[(b, n)][1]),)
-            for q in range(N_GROUPS):
-                if 0 <= ages[q] < GROUP_TILES:
-                    for bank in range(ages[q] * BANKS_PER_STEP, (ages[q] + 1) * BANKS_PER_STEP):
-                        g = bank * CHUNKS_PER_BANK // PACK
-                        if (q, g) not in acts:
-                            act = act_pool.tile([P, PACK, GROUP_TOKENS], BF16, tag="act")
-                            acts[(q, g)] = act
-                        transpose_features(q, bank, acts[(q, g)])
-            if t == CLAW_STEP:
-                claw_cols = s_psum.tile([P, BANK], F32, tag="sim")
-                pieces = D * D // P // BANK
-                for c in range(pieces):
-                    nc.tensor.matmul(
-                        out=claw_cols[:], lhsT=ones_bf16[:],
-                        rhs=claw_sb[:, c * BANK : (c + 1) * BANK],
-                        start=(c == 0), stop=(c == pieces - 1),
-                    )
-                claw_sum = const.tile([P, 1], F32)
-                nc.vector.reduce_sum(out=claw_sum[:], in_=claw_cols[:], axis=AX.X)
-                nc.vector.tensor_scalar_mul(
-                    out=neg_sharpness[:], in0=claw_sum[:], scalar1=-1.0 / (D * D * TEMPERATURE)
-                )
-
             if t + AHEAD < N_TILES:
                 x_quantised[t + AHEAD] = quantise_tokens(x_grouped[t + AHEAD])
             for q, g, grouped in feature_groups:
                 quantise_features(q, g, grouped)
             for g, half, grouped in weight_groups:
                 quantise_weights(VIS, g, half, grouped)
+            if claw_piece == CLAW_PIECES:
+                claw_sum = const.tile([P, 1], F32)
+                nc.vector.reduce_sum(out=claw_sum[:], in_=claw_cols[:], axis=AX.X)
+                nc.vector.tensor_scalar_mul(
+                    out=neg_sharpness[:], in0=claw_sum[:], scalar1=-1.0 / (D * D * TEMPERATURE)
+                )

@@ -35,8 +35,8 @@ N_GROUPS = N_TILES // GROUP_TILES
 GROUPS_PER_UNIT = TILES_PER_UNIT // GROUP_TILES
 CHUNKS_PER_BANK = BANK // GROUP_TOKENS
 BANKS_PER_STEP = 2
-AHEAD = 2
-ROW_LAG = 2 * GROUP_TILES + 3
+AHEAD = 3
+ROW_LAG = 2 * GROUP_TILES + 4
 STEPS = N_TILES + ROW_LAG + 1
 CLAW_PIECES = D * D // P // BANK
 CLAW_STEP = 6
@@ -65,18 +65,20 @@ def tile_clawmatrix_pa_kernel(
         act_pool = ctx.enter_context(tc.tile_pool(name="act", bufs=3))
         prob_pool = ctx.enter_context(tc.tile_pool(name="probs", bufs=BATCHES * TILES_PER_UNIT))
         stat_pool = ctx.enter_context(tc.tile_pool(name="stats", bufs=6))
-        x_psum = ctx.enter_context(tc.psum_pool(name="x_psum", bufs=1))
         h_psum = ctx.enter_context(tc.psum_pool(name="h_psum", bufs=HALVES))
-        y_psum = ctx.enter_context(tc.psum_pool(name="y_psum", bufs=4))
+        t_psum = ctx.enter_context(tc.psum_pool(name="t_psum", bufs=5))
         c_psum = ctx.enter_context(tc.psum_pool(name="c_psum", bufs=1))
         ctx.enter_context(tc.manual_schedule())
 
         bias_rows = const.tile([P, 2, D], BF16)
         nc.vector.memset(bias_rows[:], 0.0)
-        for s in (LANG, VIS):
-            nc.sync.dma_start(
-                out=bias_rows[0:1, s, :], in_=biases[s].rearrange("(o d) -> o d", o=1)
-            )
+
+        def load_biases():
+            for s in (LANG, VIS):
+                nc.sync.dma_start(
+                    out=bias_rows[0:1, s, :], in_=biases[s].rearrange("(o d) -> o d", o=1)
+                )
+
         affine_rows = const.tile([P, P], BF16)
         nc.vector.memset(affine_rows[:], 0.0)
 
@@ -91,13 +93,12 @@ def tile_clawmatrix_pa_kernel(
 
         x_tiles = []
 
-        def load_tokens(u):
-            s, b = u % 2, u // 2
-            for n in range(TILES_PER_UNIT):
-                first = b * TOKENS + n * P
-                x_tile = resident.tile([P, D], BF16, name="x_tile%d" % len(x_tiles))
-                nc.sync.dma_start(out=x_tile[:], in_=features[s][first : first + P, :])
-                x_tiles.append(x_tile)
+        def load_tokens(i):
+            u, n = divmod(i, TILES_PER_UNIT)
+            first = (u // 2) * TOKENS + n * P
+            x_tile = resident.tile([P, D], BF16, name="x_tile%d" % i)
+            nc.sync.dma_start(out=x_tile[:], in_=features[u % 2][first : first + P, :])
+            x_tiles.append(x_tile)
 
         def load_weights(s):
             rows_of_s = resident.tile([P, PASSES, PACK, D], BF16, name="w_rows%d" % s)
@@ -111,13 +112,15 @@ def tile_clawmatrix_pa_kernel(
             return rows_of_s
 
         w_rows = [None] * 2
+        for i in range(AHEAD):
+            load_tokens(i)
+        load_biases()
         w_rows[LANG] = load_weights(LANG)
-        load_tokens(0)
+        load_tokens(AHEAD)
         load_gains_and_shifts()
         w_rows[VIS] = load_weights(VIS)
-        load_tokens(1)
-        load_tokens(2)
-        load_tokens(3)
+        for i in range(AHEAD + 1, N_TILES):
+            load_tokens(i)
         claw_sb = resident.tile([P, D * D // P], BF16)
         nc.sync.dma_start(out=claw_sb[:], in_=claw.rearrange("(p r) c -> p (r c)", p=P))
 
@@ -166,7 +169,7 @@ def tile_clawmatrix_pa_kernel(
 
         def transpose_tokens(i):
             words = x_tiles[i][:].bitcast(F32)
-            xT = x_psum.tile([P, PACK, P], F32, tag="xT")
+            xT = t_psum.tile([P, PACK, P], F32, tag="transposed")
             for q in range(PACK):
                 nc.tensor.transpose(
                     out=xT[:, q, :], in_=words[:, q * P : (q + 1) * P], identity=ident_f32[:]
@@ -257,7 +260,7 @@ def tile_clawmatrix_pa_kernel(
             )
 
         def transpose_features(q, bank):
-            yT = y_psum.tile([P, CHUNKS_PER_BANK, GROUP_TOKENS], F32, tag="yT")
+            yT = t_psum.tile([P, CHUNKS_PER_BANK, GROUP_TOKENS], F32, tag="transposed")
             for c in range(bank * CHUNKS_PER_BANK, (bank + 1) * CHUNKS_PER_BANK):
                 for r in range(GROUP_TILES):
                     nc.tensor.transpose(
@@ -342,10 +345,11 @@ def tile_clawmatrix_pa_kernel(
             nc.sync.dma_start(out=out_rows[first : first + P, :], in_=probs[:])
 
         bias_all = const.tile([P, 2, D], F32)
-        for s in (LANG, VIS):
+
+        def spread_bias(s):
             for half in range(HALVES):
                 cols = slice(half * BANK, (half + 1) * BANK)
-                spread = h_psum.tile([P, BANK], F32, tag="acc")
+                spread = t_psum.tile([P, BANK], F32, tag="transposed")
                 nc.tensor.matmul(
                     out=spread[:], lhsT=ones_bf16[:], rhs=bias_rows[:, s, cols],
                     start=True, stop=True,
@@ -354,6 +358,12 @@ def tile_clawmatrix_pa_kernel(
 
         x_grouped = {}
         x_quantised = {}
+        first_tokens = [transpose_tokens(i) for i in range(AHEAD)]
+        for i in range(AHEAD):
+            x_grouped[i] = regroup_tokens(first_tokens[i])
+        for i in range(AHEAD - 1):
+            x_quantised[i] = quantise_tokens(x_grouped[i])
+        spread_bias(LANG)
         lang_grouped = {}
         for g in range(PASSES):
             lang_grouped[(g, 0)] = regroup_weights(LANG, g, 0, "vector")
@@ -361,11 +371,7 @@ def tile_clawmatrix_pa_kernel(
             if g > 0:
                 quantise_weights(LANG, g - 1, 1, lang_grouped[(g - 1, 1)])
             quantise_weights(LANG, g, 0, lang_grouped[(g, 0)])
-        for i in range(AHEAD):
-            x_grouped[i] = regroup_tokens(transpose_tokens(i))
         quantise_weights(LANG, PASSES - 1, 1, lang_grouped[(PASSES - 1, 1)])
-        for i in range(AHEAD):
-            x_quantised[i] = quantise_tokens(x_grouped[i])
 
         neg_sharpness = const.tile([P, 1], F32)
         claw_cols = c_psum.tile([P, BANK], F32)
@@ -384,18 +390,20 @@ def tile_clawmatrix_pa_kernel(
 
         all_rows = [(b, n) for b in range(BATCHES) for n in range(TILES_PER_UNIT)]
         projected = {0: [project(0, half) for half in range(HALVES)]}
-        affine_ps = x_psum.tile([P, P], BF16, tag="xT")
+        affine_ps = t_psum.tile([P, P], BF16, tag="transposed")
         nc.tensor.transpose(out=affine_ps[:], in_=affine_rows[:], identity=ident_bf16[:])
         affine = const.tile([P, 4 * CHUNKS], F32)
-        nc.vector.tensor_copy(out=affine[:], in_=affine_ps[:, 0 : 4 * CHUNKS])
+        nc.scalar.copy(out=affine[:], in_=affine_ps[:, 0 : 4 * CHUNKS])
+        spread_bias(VIS)
         normalised = {}
         neg_means = {}
-        ssqs = {}
+        rstds = {}
         acts = {}
         probs = {}
         neg_tops = {}
         totals = {}
         scalar_weight_groups = []
+        banks_before = {}
         for t in range(STEPS):
             ages = [t - GROUP_TILES * (q + 1) - 2 for q in range(N_GROUPS)]
             rows_now = [row for row in all_rows if row_step(row[0], row[1]) == t]
@@ -430,40 +438,38 @@ def tile_clawmatrix_pa_kernel(
             for q in range(N_GROUPS):
                 for g in range(PASSES):
                     last_bank = ((g + 1) * PACK - 1) // CHUNKS_PER_BANK
-                    if ages[q] == last_bank // BANKS_PER_STEP + 1:
+                    if ages[q] == last_bank // BANKS_PER_STEP + 2:
                         feature_groups.append((q, g, regroup_features(acts[(q, g)])))
             if 2 <= t <= N_TILES + 1:
-                rstd = inverse_deviation(ssqs[t - 2])
-                normalise(normalised[t - 2], neg_means[t - 2], rstd)
+                normalise(normalised[t - 2], neg_means[t - 2], rstds[t - 2])
             for b, n in rows_before:
                 store_probabilities(b, n, probs[(b, n)], totals[(b, n)])
 
-            if xT is not None:
-                x_grouped[t + AHEAD] = regroup_tokens(xT)
-            for q, bank in sorted(banks):
+            for q, bank in sorted(banks_before):
                 g = bank * CHUNKS_PER_BANK // PACK
                 if (q, g) not in acts:
                     act = act_pool.tile([P, PACK, GROUP_TOKENS], BF16, tag="act")
                     acts[(q, g)] = act
-                gain_and_shift(q, bank, banks[(q, bank)], acts[(q, g)])
-
-            if t < N_TILES:
-                add_bias(t, 1, projected[t][1], normalised[t], sums)
-                neg_means[t] = minus_mean(sums)
-
-            if t < N_TILES:
-                ssqs[t] = squared_deviations(normalised[t], neg_means[t])
+                gain_and_shift(q, bank, banks_before[(q, bank)], acts[(q, g)])
+            banks_before = banks
+            if 1 <= t <= N_TILES:
+                rstds[t - 1] = inverse_deviation(squared_deviations(normalised[t - 1], neg_means[t - 1]))
             for row in rows_now:
                 totals[row] = exponentials(probs[row], neg_tops[row])
+            if xT is not None:
+                x_grouped[t + AHEAD] = regroup_tokens(xT)
             weight_groups = scalar_weight_groups
             scalar_weight_groups = []
             if t < PASSES:
                 scalar_weight_groups.append((t, 1, regroup_weights(VIS, t, 1, "scalar")))
 
+            if t < N_TILES:
+                add_bias(t, 1, projected[t][1], normalised[t], sums)
+                neg_means[t] = minus_mean(sums)
             if t < PASSES:
                 weight_groups.append((t, 0, regroup_weights(VIS, t, 0, "vector")))
-            if t + AHEAD < N_TILES:
-                x_quantised[t + AHEAD] = quantise_tokens(x_grouped[t + AHEAD])
+            if t + AHEAD - 1 < N_TILES:
+                x_quantised[t + AHEAD - 1] = quantise_tokens(x_grouped[t + AHEAD - 1])
             for q, g, grouped in feature_groups:
                 quantise_features(q, g, grouped)
             for g, half, grouped in weight_groups:

@@ -26,18 +26,16 @@ CHUNKS = D // P
 RUN = 4
 
 LANG, VIS = 0, 1
-UNITS = 2 * BATCHES
+UNITS = [(LANG, 0), (LANG, 1), (VIS, 0), (VIS, 1)]
 TILES_PER_UNIT = TOKENS // P
-N_TILES = UNITS * TILES_PER_UNIT
+N_TILES = len(UNITS) * TILES_PER_UNIT
 GROUP_TILES = 2
 GROUP_TOKENS = GROUP_TILES * P
 N_GROUPS = N_TILES // GROUP_TILES
 GROUPS_PER_UNIT = TILES_PER_UNIT // GROUP_TILES
 CHUNKS_PER_BANK = BANK // GROUP_TOKENS
-BANKS_PER_STEP = 2
-AHEAD = 3
-ROW_LAG = 2 * GROUP_TILES + 4
-STEPS = N_TILES + ROW_LAG + 1
+BANKS_PER_PASS = PACK // CHUNKS_PER_BANK
+AHEAD = 4
 CLAW_PIECES = D * D // P // BANK
 CLAW_STEP = 6
 
@@ -58,13 +56,14 @@ def tile_clawmatrix_pa_kernel(
     with ExitStack() as ctx:
         const = ctx.enter_context(tc.tile_pool(name="const", bufs=1))
         resident = ctx.enter_context(tc.tile_pool(name="resident", bufs=1))
-        grouped_pool = ctx.enter_context(tc.tile_pool(name="grouped", bufs=4))
+        w_grouped_pool = ctx.enter_context(tc.tile_pool(name="w_grouped", bufs=4))
+        grouped_pool = ctx.enter_context(tc.tile_pool(name="grouped", bufs=5))
         token_pool = ctx.enter_context(tc.tile_pool(name="tokens", bufs=AHEAD + 2))
-        row_pool = ctx.enter_context(tc.tile_pool(name="rows", bufs=2 * GROUP_TILES + 3))
+        row_pool = ctx.enter_context(tc.tile_pool(name="rows", bufs=8))
         scrap_pool = ctx.enter_context(tc.tile_pool(name="scrap", bufs=1))
-        act_pool = ctx.enter_context(tc.tile_pool(name="act", bufs=3))
+        act_pool = ctx.enter_context(tc.tile_pool(name="act", bufs=6))
         prob_pool = ctx.enter_context(tc.tile_pool(name="probs", bufs=BATCHES * TILES_PER_UNIT))
-        stat_pool = ctx.enter_context(tc.tile_pool(name="stats", bufs=6))
+        stat_pool = ctx.enter_context(tc.tile_pool(name="stats", bufs=8))
         h_psum = ctx.enter_context(tc.psum_pool(name="h_psum", bufs=HALVES))
         t_psum = ctx.enter_context(tc.psum_pool(name="t_psum", bufs=5))
         c_psum = ctx.enter_context(tc.psum_pool(name="c_psum", bufs=1))
@@ -72,63 +71,77 @@ def tile_clawmatrix_pa_kernel(
 
         bias_rows = const.tile([P, 2, D], BF16)
         nc.vector.memset(bias_rows[:], 0.0)
-
-        def load_biases():
-            for s in (LANG, VIS):
-                nc.sync.dma_start(
-                    out=bias_rows[0:1, s, :], in_=biases[s].rearrange("(o d) -> o d", o=1)
-                )
-
         affine_rows = const.tile([P, P], BF16)
         nc.vector.memset(affine_rows[:], 0.0)
-
-        def load_gains_and_shifts():
-            for s in (LANG, VIS):
-                for v, vector in enumerate((gains[s], shifts[s])):
-                    first = (2 * s + v) * CHUNKS
-                    nc.sync.dma_start(
-                        out=affine_rows[first : first + CHUNKS, :],
-                        in_=vector.rearrange("(c p) -> c p", p=P),
-                    )
 
         x_tiles = []
 
         def load_tokens(i):
-            u, n = divmod(i, TILES_PER_UNIT)
-            first = (u // 2) * TOKENS + n * P
+            s, b = UNITS[i // TILES_PER_UNIT]
+            first = b * TOKENS + (i % TILES_PER_UNIT) * P
             x_tile = resident.tile([P, D], BF16, name="x_tile%d" % i)
-            nc.sync.dma_start(out=x_tile[:], in_=features[u % 2][first : first + P, :])
+            nc.sync.dma_start(out=x_tile[:], in_=features[s][first : first + P, :])
             x_tiles.append(x_tile)
 
-        def load_weights(s):
-            rows_of_s = resident.tile([P, PASSES, PACK, D], BF16, name="w_rows%d" % s)
-            for g in range(PASSES):
+        w_rows = {}
+
+        def load_weights_by_halves(s, g, half):
+            tile = resident.tile([P, PACK, BANK], BF16, name="w_rows%d_%d_%d" % (s, g, half))
+            w_rows[(s, g, half)] = tile[:]
+            for u in range(2):
+                first = g * K_PASS + u * 2 * P
                 nc.sync.dma_start(
-                    out=rows_of_s[:, g, :, :].rearrange("q (u e) d -> q u e d", u=2),
-                    in_=weights[s][g * K_PASS : (g + 1) * K_PASS, :].rearrange(
-                        "(u q e) d -> q u e d", u=2, e=2
+                    out=tile[:, 2 * u : 2 * u + 2, :],
+                    in_=weights[s][first : first + 2 * P, half * BANK : (half + 1) * BANK].rearrange(
+                        "(q e) d -> q e d", e=2
                     ),
                 )
-            return rows_of_s
 
-        w_rows = [None] * 2
-        for i in range(AHEAD):
+        def load_weights(s, g):
+            tile = resident.tile([P, PACK, D], BF16, name="w_rows%d_%d" % (s, g))
+            nc.sync.dma_start(
+                out=tile[:].rearrange("q (u e) d -> q u e d", u=2),
+                in_=weights[s][g * K_PASS : (g + 1) * K_PASS, :].rearrange(
+                    "(u q e) d -> q u e d", u=2, e=2
+                ),
+            )
+            for half in range(HALVES):
+                w_rows[(s, g, half)] = tile[:, :, half * BANK : (half + 1) * BANK]
+
+        load_tokens(0)
+        for half in range(HALVES):
+            for g in range(PASSES):
+                load_weights_by_halves(LANG, g, half)
+            load_tokens(half + 1)
+            if half == 0:
+                for s in (LANG, VIS):
+                    nc.sync.dma_start(
+                        out=bias_rows[0:1, s, :], in_=biases[s].rearrange("(o d) -> o d", o=1)
+                    )
+        load_tokens(3)
+        for s in (LANG, VIS):
+            for v, vector in enumerate((gains[s], shifts[s])):
+                first = (2 * s + v) * CHUNKS
+                nc.sync.dma_start(
+                    out=affine_rows[first : first + CHUNKS, :],
+                    in_=vector.rearrange("(c p) -> c p", p=P),
+                )
+        for i in range(4, 8):
             load_tokens(i)
-        load_biases()
-        w_rows[LANG] = load_weights(LANG)
-        load_tokens(AHEAD)
-        load_gains_and_shifts()
-        w_rows[VIS] = load_weights(VIS)
-        for i in range(AHEAD + 1, N_TILES):
+        for g in range(PASSES):
+            load_weights(VIS, g)
+        for i in range(8, N_TILES):
             load_tokens(i)
         claw_sb = resident.tile([P, D * D // P], BF16)
         nc.sync.dma_start(out=claw_sb[:], in_=claw.rearrange("(p r) c -> p (r c)", p=P))
 
         warm = const.tile([P, 1], F32)
-        nc.vector.memset(warm[:], 0.0)
-        nc.scalar.activation(out=warm[:], in_=warm[:], func=ACT.Exp)
-        minus_half = const.tile([P, 1], F32)
-        nc.vector.memset(minus_half[:], -0.5)
+        nc.vector.memset(warm[:], 1.0)
+        nc.scalar.activation(out=warm[:], in_=warm[:], func=ACT.Abs_reciprocal_sqrt)
+        zero = const.tile([P, 1], F32)
+        nc.vector.memset(zero[:], 0.0)
+        eps = const.tile([P, 1], F32)
+        nc.vector.tensor_scalar(out=eps[:], in0=zero[:], scalar1=1.0, scalar2=EPS, op0=ALU.mult, op1=ALU.add)
         ones_bf16 = const.tile([P, P], BF16)
         nc.vector.memset(ones_bf16[:], 1.0)
         ident_f32 = const.tile([P, P], F32)
@@ -142,30 +155,33 @@ def tile_clawmatrix_pa_kernel(
             ws = resident.tile([P, PASSES, D], U8, name="w_scales%d" % s, align_bytes=64)
             w_codes.append(wc)
             w_scales.append(ws)
-        for u in range(UNITS):
+        for u in range(len(UNITS)):
             ac = resident.tile([P, PASSES, TOKENS], U32, name="a_codes%d" % u, align_bytes=64)
             asc = resident.tile([P, PASSES, TOKENS], U8, name="a_scales%d" % u, align_bytes=64)
             a_codes.append(ac)
             a_scales.append(asc)
 
+        w_grouped = {}
+
         def regroup_weights(s, g, half, engine):
-            cols = slice(half * BANK, (half + 1) * BANK)
-            grouped = grouped_pool.tile([P, BANK, PACK], BF16, tag="grouped", align_bytes=64)
+            grouped = w_grouped_pool.tile([P, BANK, PACK], BF16, tag="w_grouped", align_bytes=64)
             dst = grouped[:].rearrange("p (c i) t -> p c t i", i=RUN)
-            src = w_rows[s][:, g, :, cols].rearrange("p t (c i) -> p c t i", i=RUN)
+            src = w_rows[(s, g, half)].rearrange("p t (c i) -> p c t i", i=RUN)
             if engine == "vector":
                 nc.vector.tensor_copy(out=dst, in_=src)
             else:
                 nc.scalar.copy(out=dst, in_=src)
-            return grouped
+            w_grouped[(s, g, half)] = grouped
 
-        def quantise_weights(s, g, half, grouped):
+        def quantise_weights(s, g, half):
             cols = slice(half * BANK, (half + 1) * BANK)
             nc.vector.quantize_mx(
                 out=w_codes[s][:, g, cols].bitcast(FP8X4),
                 scales=w_scales[s][:, g, cols],
-                in_=grouped[:].rearrange("p d t -> p (d t)"),
+                in_=w_grouped[(s, g, half)][:].rearrange("p d t -> p (d t)"),
             )
+
+        x_grouped, x_quantised, x_transposed = {}, {}, {}
 
         def transpose_tokens(i):
             words = x_tiles[i][:].bitcast(F32)
@@ -174,25 +190,31 @@ def tile_clawmatrix_pa_kernel(
                 nc.tensor.transpose(
                     out=xT[:, q, :], in_=words[:, q * P : (q + 1) * P], identity=ident_f32[:]
                 )
-            return xT
+            x_transposed[i] = xT
 
-        def regroup_tokens(xT):
-            x_grouped = token_pool.tile([P, PASSES, P, 2], F32, tag="x_grouped", align_bytes=64)
-            nc.scalar.copy(out=x_grouped[:], in_=xT[:].rearrange("p (g u) t -> p g t u", u=2))
-            return x_grouped
+        def regroup_tokens(i, engine="scalar"):
+            grouped = token_pool.tile([P, PASSES, P, 2], F32, tag="x_grouped", align_bytes=64)
+            src = x_transposed[i][:].rearrange("p (g u) t -> p g t u", u=2)
+            if engine == "scalar":
+                nc.scalar.copy(out=grouped[:], in_=src)
+            else:
+                nc.vector.tensor_copy(out=grouped[:], in_=src)
+            x_grouped[i] = grouped
 
-        def quantise_tokens(x_grouped):
+        def quantise_tokens(i):
             x_codes = token_pool.tile([P, PASSES * P], U32, tag="x_codes", align_bytes=64)
             x_scales = token_pool.tile([P, PASSES * P], U8, tag="x_scales", align_bytes=64)
             nc.vector.quantize_mx(
                 out=x_codes[:].bitcast(FP8X4),
                 scales=x_scales[:],
-                in_=x_grouped[:].rearrange("p g t u -> p (g t u)").bitcast(BF16),
+                in_=x_grouped[i][:].rearrange("p g t u -> p (g t u)").bitcast(BF16),
             )
-            return x_codes, x_scales
+            x_quantised[i] = (x_codes, x_scales)
+
+        projected = {}
 
         def project(i, half):
-            s = (i // TILES_PER_UNIT) % 2
+            s = UNITS[i // TILES_PER_UNIT][0]
             x_codes, x_scales = x_quantised[i]
             cols = slice(half * BANK, (half + 1) * BANK)
             acc = h_psum.tile([P, BANK], F32, tag="acc")
@@ -207,102 +229,128 @@ def tile_clawmatrix_pa_kernel(
                     start=(g == 0),
                     stop=(g == PASSES - 1),
                 )
-            return acc
+            projected[(i, half)] = acc
 
-        def add_bias(i, half, acc, h, sums):
-            s = (i // TILES_PER_UNIT) % 2
+        rows, sums, neg_means, ssqs, rstds, offsets = {}, {}, {}, {}, {}, {}
+
+        def add_bias(i, half):
+            s = UNITS[i // TILES_PER_UNIT][0]
             cols = slice(half * BANK, (half + 1) * BANK)
+            if half == 0:
+                h = row_pool.tile([P, D], F32, tag="h")
+                sums_of_i = stat_pool.tile([P, HALVES], F32, tag="sums")
+                rows[i] = h
+                sums[i] = sums_of_i
             nc.vector.scalar_tensor_tensor(
-                out=h[:, cols],
-                in0=acc[:],
+                out=rows[i][:, cols],
+                in0=projected[(i, half)][:],
                 scalar=1.0,
                 in1=bias_all[:, s, cols],
                 op0=ALU.mult,
                 op1=ALU.add,
-                accum_out=sums[:, half : half + 1],
+                accum_out=sums[i][:, half : half + 1],
             )
 
-        def minus_mean(sums):
+        def minus_mean(i):
             neg_mean = stat_pool.tile([P, 1], F32, tag="neg_mean")
             nc.vector.tensor_scalar(
                 out=neg_mean[:],
-                in0=sums[:, 0:1],
-                scalar1=sums[:, 1:2],
+                in0=sums[i][:, 0:1],
+                scalar1=sums[i][:, 1:2],
                 scalar2=-1.0 / D,
                 op0=ALU.add,
                 op1=ALU.mult,
             )
-            return neg_mean
+            neg_means[i] = neg_mean
 
-        def squared_deviations(h, neg_mean):
+        def squared_deviations(i):
             scrap = scrap_pool.tile([P, D], BF16, tag="scrap")
             ssq = stat_pool.tile([P, 1], F32, tag="ssq")
             nc.scalar.activation(
-                out=scrap[:], in_=h[:], func=ACT.Square, bias=neg_mean[:], scale=1.0,
+                out=scrap[:], in_=rows[i][:], func=ACT.Square, bias=neg_means[i][:], scale=1.0,
                 accum_out=ssq[:],
             )
-            return ssq
+            ssqs[i] = ssq
 
-        def inverse_deviation(ssq):
-            var_eps = stat_pool.tile([P, 1], F32, tag="var_eps")
-            nc.gpsimd.tensor_scalar(
-                out=var_eps[:], in0=ssq[:], scalar1=1.0 / D, scalar2=EPS,
+        def inverse_deviation(i):
+            rstd = stat_pool.tile([P, 1], F32, tag="rstd")
+            nc.scalar.activation(
+                out=rstd[:], in_=ssqs[i][:], func=ACT.Abs_reciprocal_sqrt, scale=1.0 / D, bias=eps[:]
+            )
+            rstds[i] = rstd
+
+        def offset(i):
+            off = stat_pool.tile([P, 1], F32, tag="offset")
+            nc.vector.tensor_tensor(out=off[:], in0=neg_means[i][:], in1=rstds[i][:], op=ALU.mult)
+            offsets[i] = off
+
+        def normalise(i, engine):
+            engine.tensor_scalar(
+                out=rows[i][:], in0=rows[i][:], scalar1=rstds[i][:], scalar2=offsets[i][:],
                 op0=ALU.mult, op1=ALU.add,
             )
-            rstd = stat_pool.tile([P, 1], F32, tag="rstd")
-            nc.gpsimd.tensor_tensor(out=rstd[:], in0=var_eps[:], in1=minus_half[:], op=ALU.pow)
-            return rstd
 
-        def normalise(h, neg_mean, rstd):
-            nc.vector.tensor_scalar(
-                out=h[:], in0=h[:], scalar1=neg_mean[:], scalar2=rstd[:],
-                op0=ALU.add, op1=ALU.mult,
-            )
+        row_banks, acts, grouped_acts = {}, {}, {}
 
-        def transpose_features(q, bank):
-            yT = t_psum.tile([P, CHUNKS_PER_BANK, GROUP_TOKENS], F32, tag="transposed")
-            for c in range(bank * CHUNKS_PER_BANK, (bank + 1) * CHUNKS_PER_BANK):
-                for r in range(GROUP_TILES):
+        def transpose_features(tiles, bank):
+            chunks = BANK // (len(tiles) * P)
+            yT = t_psum.tile([P, chunks, len(tiles) * P], F32, tag="transposed")
+            for c in range(chunks):
+                for r, i in enumerate(tiles):
+                    first = (bank * chunks + c) * P
                     nc.tensor.transpose(
-                        out=yT[:, c % CHUNKS_PER_BANK, r * P : (r + 1) * P],
-                        in_=normalised[q * GROUP_TILES + r][:, c * P : (c + 1) * P],
+                        out=yT[:, c, r * P : (r + 1) * P],
+                        in_=rows[i][:, first : first + P],
                         identity=ident_f32[:],
                     )
-            return yT
+            row_banks[(tiles, bank)] = yT
 
-        def gain_and_shift(q, bank, yT, act):
-            s = (q // GROUPS_PER_UNIT) % 2
-            for c in range(bank * CHUNKS_PER_BANK, (bank + 1) * CHUNKS_PER_BANK):
-                gain = affine[:, 2 * s * CHUNKS + c : 2 * s * CHUNKS + c + 1]
-                shift = affine[:, (2 * s + 1) * CHUNKS + c : (2 * s + 1) * CHUNKS + c + 1]
-                nc.scalar.activation(
-                    out=act[:, c % PACK, :], in_=yT[:, c % CHUNKS_PER_BANK, :],
-                    func=ACT.Identity, scale=gain, bias=shift,
-                )
+        def gain_and_shift(tiles, bank, engine="scalar"):
+            s = UNITS[tiles[0] // TILES_PER_UNIT][0]
+            chunks = BANK // (len(tiles) * P)
+            g = bank * chunks // PACK
+            if (tiles, g) not in acts:
+                act = act_pool.tile([P, PACK, len(tiles) * P], BF16, tag="act")
+                acts[(tiles, g)] = act
+            for c in range(chunks):
+                chunk = bank * chunks + c
+                gain = affine[:, 2 * s * CHUNKS + chunk : 2 * s * CHUNKS + chunk + 1]
+                shift = affine[:, (2 * s + 1) * CHUNKS + chunk : (2 * s + 1) * CHUNKS + chunk + 1]
+                if engine == "scalar":
+                    nc.scalar.activation(
+                        out=acts[(tiles, g)][:, chunk % PACK, :], in_=row_banks[(tiles, bank)][:, c, :],
+                        func=ACT.Identity, scale=gain, bias=shift,
+                    )
+                else:
+                    nc.vector.tensor_scalar(
+                        out=acts[(tiles, g)][:, chunk % PACK, :], in0=row_banks[(tiles, bank)][:, c, :],
+                        scalar1=gain, scalar2=shift, op0=ALU.mult, op1=ALU.add,
+                    )
 
-        def regroup_features(act):
+        def regroup_features(tiles, g):
             grouped = grouped_pool.tile(
-                [P, GROUP_TOKENS, PACK], BF16, tag="grouped", align_bytes=64
+                [P, len(tiles) * P, PACK], BF16, tag="grouped", align_bytes=64
             )
             nc.vector.tensor_scalar_max(
                 out=grouped[:].rearrange("p (c i) j -> p c j i", i=RUN),
-                in0=act[:].rearrange("p j (c i) -> p c j i", i=RUN),
+                in0=acts[(tiles, g)][:].rearrange("p j (c i) -> p c j i", i=RUN),
                 scalar1=0.0,
             )
-            return grouped
+            grouped_acts[(tiles, g)] = grouped
 
-        def quantise_features(q, g, grouped):
-            u = q // GROUPS_PER_UNIT
-            first = (q % GROUPS_PER_UNIT) * GROUP_TOKENS
-            toks = slice(first, first + GROUP_TOKENS)
+        def quantise_features(tiles, g):
+            u, first = divmod(tiles[0], TILES_PER_UNIT)
+            toks = slice(first * P, (first + len(tiles)) * P)
             nc.vector.quantize_mx(
                 out=a_codes[u][:, g, toks].bitcast(FP8X4),
                 scales=a_scales[u][:, g, toks],
-                in_=grouped[:].rearrange("p t j -> p (t j)"),
+                in_=grouped_acts[(tiles, g)][:].rearrange("p t j -> p (t j)"),
             )
 
+        sims, probs, neg_tops, totals = {}, {}, {}, {}
+
         def similarity(b, n):
-            lang_u, vis_u = 2 * b + LANG, 2 * b + VIS
+            lang_u, vis_u = b, BATCHES + b
             sim = h_psum.tile([P, TOKENS], F32, tag="acc")
             toks = slice(n * P, (n + 1) * P)
             for g in range(PASSES):
@@ -315,63 +363,89 @@ def tile_clawmatrix_pa_kernel(
                     start=(g == 0),
                     stop=(g == PASSES - 1),
                 )
-            return sim
+            sims[(b, n)] = sim
 
-        def negated_logits(sim):
-            probs = prob_pool.tile([P, TOKENS], F32, tag="probs")
+        def negated_logits(b, n):
+            prob = prob_pool.tile([P, TOKENS], F32, tag="probs")
             neg_top = stat_pool.tile([P, 1], F32, tag="neg_top")
             nc.vector.tensor_scalar(
-                out=probs[:], in0=sim[:], scalar1=neg_sharpness[:], scalar2=None,
+                out=prob[:], in0=sims[(b, n)][:], scalar1=neg_sharpness[:], scalar2=None,
                 op0=ALU.mult, op1=ALU.min, accum_out=neg_top[:],
             )
-            return probs, neg_top
+            probs[(b, n)] = prob
+            neg_tops[(b, n)] = neg_top
 
-        def exponentials(probs, neg_top):
+        def exponentials(b, n):
             total = stat_pool.tile([P, 1], F32, tag="total")
             nc.scalar.activation(
-                out=probs[:], in_=probs[:], func=ACT.Exp, bias=neg_top[:], scale=-1.0,
-                accum_out=total[:],
+                out=probs[(b, n)][:], in_=probs[(b, n)][:], func=ACT.Exp, bias=neg_tops[(b, n)][:],
+                scale=-1.0, accum_out=total[:],
             )
-            return total
+            totals[(b, n)] = total
 
-        def store_probabilities(b, n, probs, total):
+        def store_probabilities(b, n, engine="vector"):
             inv_total = stat_pool.tile([P, 1], F32, tag="inv_total")
-            nc.vector.reciprocal(out=inv_total[:], in_=total[:])
-            nc.gpsimd.tensor_scalar(
-                out=probs[:], in0=probs[:], scalar1=inv_total[:], scalar2=0.0,
-                op0=ALU.mult, op1=ALU.add,
-            )
+            nc.vector.reciprocal(out=inv_total[:], in_=totals[(b, n)][:])
+            prob = probs[(b, n)]
+            if engine == "vector":
+                nc.vector.tensor_scalar(
+                    out=prob[:], in0=prob[:], scalar1=inv_total[:], scalar2=None, op0=ALU.mult
+                )
+            elif engine == "gpsimd":
+                nc.gpsimd.tensor_scalar(
+                    out=prob[:], in0=prob[:], scalar1=inv_total[:], scalar2=0.0,
+                    op0=ALU.mult, op1=ALU.add,
+                )
+            else:
+                nc.scalar.activation(out=prob[:], in_=prob[:], func=ACT.Copy, scale=inv_total[:])
             first = b * TOKENS + n * P
-            nc.sync.dma_start(out=out_rows[first : first + P, :], in_=probs[:])
+            nc.sync.dma_start(out=out_rows[first : first + P, :], in_=prob[:])
 
-        bias_all = const.tile([P, 2, D], F32)
+        bias_all = const.tile([P, 2, D], BF16)
 
         def spread_bias(s):
+            spread = t_psum.tile([P, D], BF16, tag="transposed")
             for half in range(HALVES):
                 cols = slice(half * BANK, (half + 1) * BANK)
-                spread = t_psum.tile([P, BANK], F32, tag="transposed")
                 nc.tensor.matmul(
-                    out=spread[:], lhsT=ones_bf16[:], rhs=bias_rows[:, s, cols],
+                    out=spread[:, cols], lhsT=ones_bf16[:], rhs=bias_rows[:, s, cols],
                     start=True, stop=True,
                 )
-                nc.scalar.copy(out=bias_all[:, s, cols], in_=spread[:])
+            nc.scalar.copy(out=bias_all[:, s, :], in_=spread[:])
 
-        x_grouped = {}
-        x_quantised = {}
-        first_tokens = [transpose_tokens(i) for i in range(AHEAD)]
-        for i in range(AHEAD):
-            x_grouped[i] = regroup_tokens(first_tokens[i])
-        for i in range(AHEAD - 1):
-            x_quantised[i] = quantise_tokens(x_grouped[i])
+        affine = const.tile([P, 4 * CHUNKS], F32)
+
+        def spread_affine():
+            affine_ps = t_psum.tile([P, P], BF16, tag="transposed")
+            nc.tensor.transpose(out=affine_ps[:], in_=affine_rows[:], identity=ident_bf16[:])
+            nc.scalar.copy(out=affine[:], in_=affine_ps[:, 0 : 4 * CHUNKS])
+
+        transpose_tokens(0)
+        regroup_tokens(0)
+        quantise_tokens(0)
+        regroup_weights(LANG, 0, 0, "vector")
+        regroup_weights(LANG, 1, 0, "scalar")
         spread_bias(LANG)
-        lang_grouped = {}
-        for g in range(PASSES):
-            lang_grouped[(g, 0)] = regroup_weights(LANG, g, 0, "vector")
-            lang_grouped[(g, 1)] = regroup_weights(LANG, g, 1, "scalar")
-            if g > 0:
-                quantise_weights(LANG, g - 1, 1, lang_grouped[(g - 1, 1)])
-            quantise_weights(LANG, g, 0, lang_grouped[(g, 0)])
-        quantise_weights(LANG, PASSES - 1, 1, lang_grouped[(PASSES - 1, 1)])
+        quantise_weights(LANG, 0, 0)
+        transpose_tokens(1)
+        regroup_tokens(1)
+        regroup_weights(LANG, 0, 1, "vector")
+        regroup_weights(LANG, 1, 1, "scalar")
+        quantise_weights(LANG, 1, 0)
+        project(0, 0)
+        quantise_tokens(1)
+        quantise_weights(LANG, 0, 1)
+        project(1, 0)
+        transpose_tokens(2)
+        regroup_tokens(2)
+        add_bias(0, 0)
+        add_bias(1, 0)
+        quantise_weights(LANG, 1, 1)
+        project(0, 1)
+        project(1, 1)
+        spread_affine()
+        transpose_tokens(3)
+        regroup_tokens(3)
 
         neg_sharpness = const.tile([P, 1], F32)
         claw_cols = c_psum.tile([P, BANK], F32)
@@ -383,100 +457,143 @@ def tile_clawmatrix_pa_kernel(
                 start=(piece == 0), stop=(piece == CLAW_PIECES - 1),
             )
 
-        def row_step(b, n):
-            if b == 0:
-                return N_TILES + n
-            return (2 * b + VIS) * TILES_PER_UNIT + n + ROW_LAG
+        def finish_claw():
+            claw_sum = const.tile([P, 1], F32)
+            nc.vector.reduce_sum(out=claw_sum[:], in_=claw_cols[:], axis=AX.X)
+            nc.vector.tensor_scalar_mul(
+                out=neg_sharpness[:], in0=claw_sum[:], scalar1=-1.0 / (D * D * TEMPERATURE)
+            )
 
-        all_rows = [(b, n) for b in range(BATCHES) for n in range(TILES_PER_UNIT)]
-        projected = {0: [project(0, half) for half in range(HALVES)]}
-        affine_ps = t_psum.tile([P, P], BF16, tag="transposed")
-        nc.tensor.transpose(out=affine_ps[:], in_=affine_rows[:], identity=ident_bf16[:])
-        affine = const.tile([P, 4 * CHUNKS], F32)
-        nc.scalar.copy(out=affine[:], in_=affine_ps[:, 0 : 4 * CHUNKS])
-        spread_bias(VIS)
-        normalised = {}
-        neg_means = {}
-        rstds = {}
-        acts = {}
-        probs = {}
-        neg_tops = {}
-        totals = {}
-        scalar_weight_groups = []
-        banks_before = {}
-        for t in range(STEPS):
-            ages = [t - GROUP_TILES * (q + 1) - 2 for q in range(N_GROUPS)]
-            rows_now = [row for row in all_rows if row_step(row[0], row[1]) == t]
-            rows_before = [row for row in all_rows if row_step(row[0], row[1]) == t - 1]
-            transposing = [q for q in range(N_GROUPS) if 0 <= ages[q] < GROUP_TILES]
+        PAIRS = [(2 * q, 2 * q + 1) for q in range(7)]
+        vis_blocks = [(0, 0), (1, 0), (0, 1), (1, 1)]
+        VIS_STEP = {1: 0, 2: 1, 3: 2, 5: 3}
+        VIS_ENG = ["vector", "scalar", "vector", "scalar"]
+
+        def at(t, lag):
+            q, g = divmod(t - lag, 2)
+            return (PAIRS[q], g) if 0 <= q < len(PAIRS) else None
+
+        pending_w = []
+        for t in range(N_TILES):
+            if t >= 1:
+                squared_deviations(t - 1)
+            before = at(t, 4)
+            if before:
+                gain_and_shift(before[0], 2 * before[1])
+            if t >= 1:
+                inverse_deviation(t - 1)
+            if before:
+                gain_and_shift(before[0], 2 * before[1] + 1)
+            tok = t + AHEAD - 1
+            tok_engine = "scalar" if t < 3 or tok % 3 else "vector"
+            if t >= 1 and tok < N_TILES and tok_engine == "scalar":
+                regroup_tokens(tok)
+            if t >= 2:
+                offset(t - 2)
+            if t > 1:
+                add_bias(t, 0)
+            add_bias(t, 1)
+            if t >= 2:
+                normalise(t - 2, nc.gpsimd)
+            feat = at(t, 5)
+            if feat:
+                regroup_features(*feat)
+            minus_mean(t)
+            if t >= 1 and tok < N_TILES and tok_engine == "vector":
+                regroup_tokens(tok, "vector")
+            if t + 2 < N_TILES:
+                quantise_tokens(t + 2)
+            if feat:
+                quantise_features(*feat)
+            for w in pending_w:
+                quantise_weights(VIS, *w)
+            pending_w = []
+            if t in VIS_STEP:
+                k = VIS_STEP[t]
+                regroup_weights(VIS, vis_blocks[k][0], vis_blocks[k][1], VIS_ENG[k])
+                pending_w.append(vis_blocks[k])
             claw_piece = 2 * (t - CLAW_STEP)
-
-            sims = [similarity(b, n) for b, n in rows_now]
-            banks = {}
-            xT = None
-            for half in range(HALVES):
-                if t + 1 < N_TILES:
-                    if half == 0:
-                        projected[t + 1] = []
-                    projected[t + 1].append(project(t + 1, half))
-                if 0 <= claw_piece < CLAW_PIECES:
-                    add_claw_block(claw_piece + half)
-                for q in transposing:
-                    bank = ages[q] * BANKS_PER_STEP + half
-                    banks[(q, bank)] = transpose_features(q, bank)
-                if half == 0 and t + AHEAD < N_TILES:
-                    xT = transpose_tokens(t + AHEAD)
-
-            for row, sim in zip(rows_now, sims):
-                probs[row], neg_tops[row] = negated_logits(sim)
-            if t < N_TILES:
-                h = row_pool.tile([P, D], F32, tag="h")
-                sums = stat_pool.tile([P, HALVES], F32, tag="sums")
-                normalised[t] = h
-                add_bias(t, 0, projected[t][0], h, sums)
-            feature_groups = []
-            for q in range(N_GROUPS):
-                for g in range(PASSES):
-                    last_bank = ((g + 1) * PACK - 1) // CHUNKS_PER_BANK
-                    if ages[q] == last_bank // BANKS_PER_STEP + 2:
-                        feature_groups.append((q, g, regroup_features(acts[(q, g)])))
-            if 2 <= t <= N_TILES + 1:
-                normalise(normalised[t - 2], neg_means[t - 2], rstds[t - 2])
-            for b, n in rows_before:
-                store_probabilities(b, n, probs[(b, n)], totals[(b, n)])
-
-            for q, bank in sorted(banks_before):
-                g = bank * CHUNKS_PER_BANK // PACK
-                if (q, g) not in acts:
-                    act = act_pool.tile([P, PACK, GROUP_TOKENS], BF16, tag="act")
-                    acts[(q, g)] = act
-                gain_and_shift(q, bank, banks_before[(q, bank)], acts[(q, g)])
-            banks_before = banks
-            if 1 <= t <= N_TILES:
-                rstds[t - 1] = inverse_deviation(squared_deviations(normalised[t - 1], neg_means[t - 1]))
-            for row in rows_now:
-                totals[row] = exponentials(probs[row], neg_tops[row])
-            if xT is not None:
-                x_grouped[t + AHEAD] = regroup_tokens(xT)
-            weight_groups = scalar_weight_groups
-            scalar_weight_groups = []
-            if t < PASSES:
-                scalar_weight_groups.append((t, 1, regroup_weights(VIS, t, 1, "scalar")))
-
-            if t < N_TILES:
-                add_bias(t, 1, projected[t][1], normalised[t], sums)
-                neg_means[t] = minus_mean(sums)
-            if t < PASSES:
-                weight_groups.append((t, 0, regroup_weights(VIS, t, 0, "vector")))
-            if t + AHEAD - 1 < N_TILES:
-                x_quantised[t + AHEAD - 1] = quantise_tokens(x_grouped[t + AHEAD - 1])
-            for q, g, grouped in feature_groups:
-                quantise_features(q, g, grouped)
-            for g, half, grouped in weight_groups:
-                quantise_weights(VIS, g, half, grouped)
             if claw_piece == CLAW_PIECES:
-                claw_sum = const.tile([P, 1], F32)
-                nc.vector.reduce_sum(out=claw_sum[:], in_=claw_cols[:], axis=AX.X)
-                nc.vector.tensor_scalar_mul(
-                    out=neg_sharpness[:], in0=claw_sum[:], scalar1=-1.0 / (D * D * TEMPERATURE)
-                )
+                finish_claw()
+            if 1 <= t and t + 1 < N_TILES:
+                project(t + 1, 0)
+                project(t + 1, 1)
+            if 0 <= claw_piece < CLAW_PIECES:
+                add_claw_block(claw_piece)
+                add_claw_block(claw_piece + 1)
+            now = at(t, 3)
+            if now:
+                transpose_features(now[0], 2 * now[1])
+                transpose_features(now[0], 2 * now[1] + 1)
+            if t + AHEAD < N_TILES:
+                transpose_tokens(t + AHEAD)
+            if t == 5:
+                spread_bias(VIS)
+        T14, T15 = (14,), (15,)
+        P5, P6 = (10, 11), (12, 13)
+        offset(14)
+        normalise(14, nc.vector)
+        squared_deviations(15)
+        inverse_deviation(15)
+        transpose_features(P6, 2)
+        transpose_features(P6, 3)
+        similarity(0, 0)
+        similarity(0, 1)
+        gain_and_shift(P6, 0)
+        gain_and_shift(P6, 1)
+        regroup_features(P5, 1)
+        negated_logits(0, 0)
+        quantise_features(P5, 1)
+        offset(15)
+        normalise(15, nc.vector)
+        transpose_features(T14, 0)
+        transpose_features(T14, 1)
+        negated_logits(0, 1)
+        gain_and_shift(P6, 2)
+        gain_and_shift(P6, 3)
+        exponentials(0, 0)
+        regroup_features(P6, 0)
+        transpose_features(T15, 0)
+        transpose_features(T15, 1)
+        gain_and_shift(T14, 0)
+        gain_and_shift(T14, 1)
+        quantise_features(P6, 0)
+        gain_and_shift(T15, 1, "vector")
+        gain_and_shift(T15, 0)
+        exponentials(0, 1)
+        regroup_features(P6, 1)
+        similarity(0, 2)
+        similarity(0, 3)
+        negated_logits(0, 2)
+        quantise_features(P6, 1)
+        regroup_features(T14, 0)
+        regroup_features(T14, 1)
+        quantise_features(T14, 0)
+        quantise_features(T14, 1)
+        regroup_features(T15, 1)
+        regroup_features(T15, 0)
+        negated_logits(0, 3)
+        quantise_features(T15, 1)
+        quantise_features(T15, 0)
+        store_probabilities(0, 0, "gpsimd")
+        store_probabilities(0, 1, "gpsimd")
+        exponentials(0, 2)
+        similarity(1, 0)
+        similarity(1, 1)
+        negated_logits(1, 0)
+        exponentials(0, 3)
+        negated_logits(1, 1)
+        store_probabilities(0, 2, "gpsimd")
+        similarity(1, 2)
+        similarity(1, 3)
+        exponentials(1, 0)
+        exponentials(1, 1)
+        negated_logits(1, 2)
+        store_probabilities(0, 3, "gpsimd")
+        negated_logits(1, 3)
+        exponentials(1, 2)
+        store_probabilities(1, 0)
+        exponentials(1, 3)
+        store_probabilities(1, 1)
+        store_probabilities(1, 2)
+        store_probabilities(1, 3)

@@ -290,6 +290,12 @@ def tile_clawmatrix_pa_kernel(
                 op0=ALU.mult, op1=ALU.add,
             )
 
+        def normalise_now(i, engine):
+            engine.tensor_scalar(
+                out=rows[i][:], in0=rows[i][:], scalar1=neg_means[i][:], scalar2=rstds[i][:],
+                op0=ALU.add, op1=ALU.mult,
+            )
+
         row_banks, acts, grouped_acts = {}, {}, {}
 
         def transpose_features(tiles, bank):
@@ -327,15 +333,16 @@ def tile_clawmatrix_pa_kernel(
                         scalar1=gain, scalar2=shift, op0=ALU.mult, op1=ALU.add,
                     )
 
-        def regroup_features(tiles, g):
+        def regroup_features(tiles, g, engine="vector"):
             grouped = grouped_pool.tile(
                 [P, len(tiles) * P, PACK], BF16, tag="grouped", align_bytes=64
             )
-            nc.vector.tensor_scalar_max(
-                out=grouped[:].rearrange("p (c i) j -> p c j i", i=RUN),
-                in0=acts[(tiles, g)][:].rearrange("p j (c i) -> p c j i", i=RUN),
-                scalar1=0.0,
-            )
+            dst = grouped[:].rearrange("p (c i) j -> p c j i", i=RUN)
+            src = acts[(tiles, g)][:].rearrange("p j (c i) -> p c j i", i=RUN)
+            if engine == "vector":
+                nc.vector.tensor_scalar_max(out=dst, in0=src, scalar1=0.0)
+            else:
+                nc.scalar.activation(out=dst, in_=src, func=ACT.Relu)
             grouped_acts[(tiles, g)] = grouped
 
         def quantise_features(tiles, g):
@@ -349,9 +356,12 @@ def tile_clawmatrix_pa_kernel(
 
         sims, probs, neg_tops, totals = {}, {}, {}, {}
 
-        def similarity(b, n):
+        def similarity(b, n, pool="h"):
             lang_u, vis_u = b, BATCHES + b
-            sim = h_psum.tile([P, TOKENS], F32, tag="acc")
+            if pool == "h":
+                sim = h_psum.tile([P, TOKENS], F32, tag="acc")
+            else:
+                sim = t_psum.tile([P, TOKENS], F32, tag="transposed")
             toks = slice(n * P, (n + 1) * P)
             for g in range(PASSES):
                 nc.tensor.matmul_mx(
@@ -383,10 +393,16 @@ def tile_clawmatrix_pa_kernel(
             )
             totals[(b, n)] = total
 
-        def store_probabilities(b, n, engine="vector"):
+        inv_totals = {}
+
+        def invert_total(b, n):
             inv_total = stat_pool.tile([P, 1], F32, tag="inv_total")
             nc.vector.reciprocal(out=inv_total[:], in_=totals[(b, n)][:])
+            inv_totals[(b, n)] = inv_total
+
+        def store_probabilities(b, n, engine="vector"):
             prob = probs[(b, n)]
+            inv_total = inv_totals[(b, n)]
             if engine == "vector":
                 nc.vector.tensor_scalar(
                     out=prob[:], in0=prob[:], scalar1=inv_total[:], scalar2=None, op0=ALU.mult
@@ -448,14 +464,14 @@ def tile_clawmatrix_pa_kernel(
         regroup_tokens(3)
 
         neg_sharpness = const.tile([P, 1], F32)
-        claw_cols = c_psum.tile([P, BANK], F32)
+        claw_cols = c_psum.tile([P, P], F32)
 
         def add_claw_block(piece):
-            nc.tensor.matmul(
-                out=claw_cols[:], lhsT=ones_bf16[:],
-                rhs=claw_sb[:, piece * BANK : (piece + 1) * BANK],
-                start=(piece == 0), stop=(piece == CLAW_PIECES - 1),
-            )
+            for k in range(piece * (BANK // P), (piece + 1) * (BANK // P)):
+                nc.tensor.matmul(
+                    out=claw_cols[:], lhsT=ones_bf16[:], rhs=claw_sb[:, k * P : (k + 1) * P],
+                    start=(k == 0), stop=(k == CLAW_PIECES * (BANK // P) - 1),
+                )
 
         def finish_claw():
             claw_sum = const.tile([P, 1], F32)
@@ -531,69 +547,75 @@ def tile_clawmatrix_pa_kernel(
                 spread_bias(VIS)
         T14, T15 = (14,), (15,)
         P5, P6 = (10, 11), (12, 13)
-        offset(14)
-        normalise(14, nc.vector)
         squared_deviations(15)
         inverse_deviation(15)
-        transpose_features(P6, 2)
-        transpose_features(P6, 3)
-        similarity(0, 0)
-        similarity(0, 1)
+        normalise_now(14, nc.vector)
         gain_and_shift(P6, 0)
         gain_and_shift(P6, 1)
         regroup_features(P5, 1)
-        negated_logits(0, 0)
-        quantise_features(P5, 1)
-        offset(15)
-        normalise(15, nc.vector)
+        transpose_features(P6, 2)
+        transpose_features(P6, 3)
         transpose_features(T14, 0)
         transpose_features(T14, 1)
-        negated_logits(0, 1)
+        similarity(0, 0)
+        quantise_features(P5, 1)
         gain_and_shift(P6, 2)
         gain_and_shift(P6, 3)
-        exponentials(0, 0)
+        normalise_now(15, nc.vector)
+        gain_and_shift(T14, 0)
+        gain_and_shift(T14, 1, "vector")
         regroup_features(P6, 0)
+        similarity(0, 1)
         transpose_features(T15, 0)
         transpose_features(T15, 1)
-        gain_and_shift(T14, 0)
-        gain_and_shift(T14, 1)
-        quantise_features(P6, 0)
-        gain_and_shift(T15, 1, "vector")
         gain_and_shift(T15, 0)
-        exponentials(0, 1)
+        gain_and_shift(T15, 1)
+        negated_logits(0, 0)
+        quantise_features(P6, 0)
         regroup_features(P6, 1)
+        negated_logits(0, 1)
+        quantise_features(P6, 1)
+        regroup_features(T14, 1)
+        regroup_features(T14, 0)
         similarity(0, 2)
         similarity(0, 3)
-        negated_logits(0, 2)
-        quantise_features(P6, 1)
-        regroup_features(T14, 0)
-        regroup_features(T14, 1)
-        quantise_features(T14, 0)
+        exponentials(0, 0)
+        exponentials(0, 1)
         quantise_features(T14, 1)
-        regroup_features(T15, 1)
+        quantise_features(T14, 0)
+        negated_logits(0, 2)
+        similarity(1, 0, "t")
+        similarity(1, 1, "t")
+        similarity(1, 2, "t")
         regroup_features(T15, 0)
+        regroup_features(T15, 1)
         negated_logits(0, 3)
-        quantise_features(T15, 1)
+        exponentials(0, 2)
+        exponentials(0, 3)
         quantise_features(T15, 0)
+        quantise_features(T15, 1)
+        similarity(1, 3, "t")
+        invert_total(0, 0)
+        negated_logits(1, 0)
+        invert_total(0, 1)
+        negated_logits(1, 1)
         store_probabilities(0, 0, "gpsimd")
         store_probabilities(0, 1, "gpsimd")
-        exponentials(0, 2)
-        similarity(1, 0)
-        similarity(1, 1)
-        negated_logits(1, 0)
-        exponentials(0, 3)
-        negated_logits(1, 1)
-        store_probabilities(0, 2, "gpsimd")
-        similarity(1, 2)
-        similarity(1, 3)
         exponentials(1, 0)
         exponentials(1, 1)
+        invert_total(0, 2)
         negated_logits(1, 2)
-        store_probabilities(0, 3, "gpsimd")
+        invert_total(0, 3)
         negated_logits(1, 3)
+        store_probabilities(0, 2, "gpsimd")
         exponentials(1, 2)
-        store_probabilities(1, 0)
         exponentials(1, 3)
+        store_probabilities(0, 3)
+        invert_total(1, 0)
+        invert_total(1, 1)
+        store_probabilities(1, 0)
         store_probabilities(1, 1)
+        invert_total(1, 2)
+        invert_total(1, 3)
         store_probabilities(1, 2)
         store_probabilities(1, 3)

@@ -70,9 +70,9 @@ def tile_clawmatrix_pa_kernel(
         ctx.enter_context(tc.manual_schedule())
 
         bias_rows = const.tile([P, 2, D], BF16)
-        nc.vector.memset(bias_rows[:], 0.0)
+        nc.vector.memset(bias_rows[:].rearrange("p s d -> p (s d)").bitcast(U32), 0)
         affine_rows = const.tile([P, P], BF16)
-        nc.vector.memset(affine_rows[:], 0.0)
+        nc.vector.memset(affine_rows[:].bitcast(U32), 0)
 
         x_tiles = []
 
@@ -108,17 +108,17 @@ def tile_clawmatrix_pa_kernel(
             for half in range(HALVES):
                 w_rows[(s, g, half)] = tile[:, :, half * BANK : (half + 1) * BANK]
 
-        load_tokens(0)
         for half in range(HALVES):
             for g in range(PASSES):
                 load_weights_by_halves(LANG, g, half)
-            load_tokens(half + 1)
             if half == 0:
+                load_tokens(0)
                 for s in (LANG, VIS):
                     nc.sync.dma_start(
                         out=bias_rows[0:1, s, :], in_=biases[s].rearrange("(o d) -> o d", o=1)
                     )
-        load_tokens(3)
+        for i in range(1, 4):
+            load_tokens(i)
         for s in (LANG, VIS):
             for v, vector in enumerate((gains[s], shifts[s])):
                 first = (2 * s + v) * CHUNKS
@@ -436,31 +436,31 @@ def tile_clawmatrix_pa_kernel(
             nc.tensor.transpose(out=affine_ps[:], in_=affine_rows[:], identity=ident_bf16[:])
             nc.scalar.copy(out=affine[:], in_=affine_ps[:, 0 : 4 * CHUNKS])
 
+        regroup_weights(LANG, 0, 0, "vector")
+        regroup_weights(LANG, 1, 0, "vector")
         transpose_tokens(0)
         regroup_tokens(0)
-        quantise_tokens(0)
-        regroup_weights(LANG, 0, 0, "vector")
-        regroup_weights(LANG, 1, 0, "scalar")
         spread_bias(LANG)
         quantise_weights(LANG, 0, 0)
-        transpose_tokens(1)
-        regroup_tokens(1)
-        regroup_weights(LANG, 0, 1, "vector")
-        regroup_weights(LANG, 1, 1, "scalar")
+        regroup_weights(LANG, 0, 1, "scalar")
+        quantise_tokens(0)
         quantise_weights(LANG, 1, 0)
         project(0, 0)
-        quantise_tokens(1)
-        quantise_weights(LANG, 0, 1)
-        project(1, 0)
+        transpose_tokens(1)
+        regroup_tokens(1)
+        regroup_weights(LANG, 1, 1, "vector")
         transpose_tokens(2)
         regroup_tokens(2)
+        transpose_tokens(3)
         add_bias(0, 0)
-        add_bias(1, 0)
+        quantise_weights(LANG, 0, 1)
+        quantise_tokens(1)
         quantise_weights(LANG, 1, 1)
+        project(1, 0)
         project(0, 1)
+        add_bias(1, 0)
         project(1, 1)
         spread_affine()
-        transpose_tokens(3)
         regroup_tokens(3)
 
         neg_sharpness = const.tile([P, 1], F32)

@@ -56,10 +56,10 @@ def tile_clawmatrix_pa_kernel(
     with ExitStack() as ctx:
         const = ctx.enter_context(tc.tile_pool(name="const", bufs=1))
         resident = ctx.enter_context(tc.tile_pool(name="resident", bufs=1))
-        w_grouped_pool = ctx.enter_context(tc.tile_pool(name="w_grouped", bufs=4))
+        w_grouped_pool = ctx.enter_context(tc.tile_pool(name="w_grouped", bufs=3))
         grouped_pool = ctx.enter_context(tc.tile_pool(name="grouped", bufs=5))
         token_pool = ctx.enter_context(tc.tile_pool(name="tokens", bufs=AHEAD + 2))
-        row_pool = ctx.enter_context(tc.tile_pool(name="rows", bufs=8))
+        row_pool = ctx.enter_context(tc.tile_pool(name="rows", bufs=7))
         scrap_pool = ctx.enter_context(tc.tile_pool(name="scrap", bufs=1))
         act_pool = ctx.enter_context(tc.tile_pool(name="act", bufs=6))
         prob_pool = ctx.enter_context(tc.tile_pool(name="probs", bufs=BATCHES * TILES_PER_UNIT))
@@ -69,8 +69,12 @@ def tile_clawmatrix_pa_kernel(
         c_psum = ctx.enter_context(tc.psum_pool(name="c_psum", bufs=1))
         ctx.enter_context(tc.manual_schedule())
 
-        bias_rows = const.tile([P, 2, D], BF16)
-        nc.vector.memset(bias_rows[:].rearrange("p s d -> p (s d)").bitcast(U32), 0)
+        bias_rows = const.tile([P, D], BF16)
+        nc.vector.memset(bias_rows[:].bitcast(U32), 0)
+        bias_tiles = [
+            const.tile([P, D], BF16, name="bias_lang"),
+            const.tile([P, D], BF16, name="bias_vis"),
+        ]
         affine_rows = const.tile([P, P], BF16)
         nc.vector.memset(affine_rows[:].bitcast(U32), 0)
 
@@ -113,10 +117,9 @@ def tile_clawmatrix_pa_kernel(
                 load_weights_by_halves(LANG, g, half)
             if half == 0:
                 load_tokens(0)
-                for s in (LANG, VIS):
-                    nc.sync.dma_start(
-                        out=bias_rows[0:1, s, :], in_=biases[s].rearrange("(o d) -> o d", o=1)
-                    )
+                nc.sync.dma_start(
+                    out=bias_rows[0:1, :], in_=biases[LANG].rearrange("(o d) -> o d", o=1)
+                )
         for i in range(1, 4):
             load_tokens(i)
         for s in (LANG, VIS):
@@ -132,6 +135,7 @@ def tile_clawmatrix_pa_kernel(
             load_weights(VIS, g)
         for i in range(8, N_TILES):
             load_tokens(i)
+        nc.sync.dma_start(out=bias_tiles[VIS][:], in_=biases[VIS].partition_broadcast(P))
         claw_sb = resident.tile([P, D * D // P], BF16)
         nc.sync.dma_start(out=claw_sb[:], in_=claw.rearrange("(p r) c -> p (r c)", p=P))
 
@@ -172,6 +176,45 @@ def tile_clawmatrix_pa_kernel(
             else:
                 nc.scalar.copy(out=dst, in_=src)
             w_grouped[(s, g, half)] = grouped
+
+        PIECE = BANK // 2
+
+        def regroup_piece(s, g, k, engine):
+            grouped = w_grouped_pool.tile([P, PIECE, PACK], BF16, tag="w_piece", align_bytes=64)
+            half, first = divmod(k * PIECE, BANK)
+            dst = grouped[:].rearrange("p (c i) t -> p c t i", i=RUN)
+            src = w_rows[(s, g, half)][:, :, first : first + PIECE].rearrange("p t (c i) -> p c t i", i=RUN)
+            if engine == "vector":
+                nc.vector.tensor_copy(out=dst, in_=src)
+            else:
+                nc.scalar.copy(out=dst, in_=src)
+            w_grouped[(s, g, k, "piece")] = grouped
+
+        w_in_psum = {}
+
+        def interleave_piece(s, g, k):
+            spread = c_psum.tile([P, PIECE, PACK], BF16, tag="side")
+            for part in range(PIECE // P):
+                half, first = divmod(k * PIECE + part * P, BANK)
+                nc.tensor.matmul(
+                    out=spread[:, part * P : (part + 1) * P, :], lhsT=ident_bf16[:],
+                    rhs=w_rows[(s, g, half)][:, :, first : first + P].rearrange("p t d -> p d t"),
+                    start=True, stop=True,
+                )
+            w_in_psum[(s, g, k)] = spread
+
+        def copy_piece(s, g, k):
+            grouped = w_grouped_pool.tile([P, PIECE, PACK], BF16, tag="w_piece", align_bytes=64)
+            nc.scalar.copy(out=grouped[:], in_=w_in_psum[(s, g, k)][:])
+            w_grouped[(s, g, k, "piece")] = grouped
+
+        def quantise_piece(s, g, k):
+            cols = slice(k * PIECE, (k + 1) * PIECE)
+            nc.vector.quantize_mx(
+                out=w_codes[s][:, g, cols].bitcast(FP8X4),
+                scales=w_scales[s][:, g, cols],
+                in_=w_grouped[(s, g, k, "piece")][:].rearrange("p d t -> p (d t)"),
+            )
 
         def quantise_weights(s, g, half):
             cols = slice(half * BANK, (half + 1) * BANK)
@@ -245,7 +288,7 @@ def tile_clawmatrix_pa_kernel(
                 out=rows[i][:, cols],
                 in0=projected[(i, half)][:],
                 scalar=1.0,
-                in1=bias_all[:, s, cols],
+                in1=bias_tiles[s][:, cols],
                 op0=ALU.mult,
                 op1=ALU.add,
                 accum_out=sums[i][:, half : half + 1],
@@ -417,17 +460,15 @@ def tile_clawmatrix_pa_kernel(
             first = b * TOKENS + n * P
             nc.sync.dma_start(out=out_rows[first : first + P, :], in_=prob[:])
 
-        bias_all = const.tile([P, 2, D], BF16)
-
-        def spread_bias(s):
+        def spread_bias():
             spread = t_psum.tile([P, D], BF16, tag="transposed")
             for half in range(HALVES):
                 cols = slice(half * BANK, (half + 1) * BANK)
                 nc.tensor.matmul(
-                    out=spread[:, cols], lhsT=ones_bf16[:], rhs=bias_rows[:, s, cols],
+                    out=spread[:, cols], lhsT=ones_bf16[:], rhs=bias_rows[:, cols],
                     start=True, stop=True,
                 )
-            nc.scalar.copy(out=bias_all[:, s, :], in_=spread[:])
+            nc.scalar.copy(out=bias_tiles[LANG][:], in_=spread[:])
 
         affine = const.tile([P, 4 * CHUNKS], F32)
 
@@ -440,7 +481,7 @@ def tile_clawmatrix_pa_kernel(
         regroup_weights(LANG, 1, 0, "vector")
         transpose_tokens(0)
         regroup_tokens(0)
-        spread_bias(LANG)
+        spread_bias()
         quantise_weights(LANG, 0, 0)
         regroup_weights(LANG, 0, 1, "scalar")
         quantise_tokens(0)
@@ -464,32 +505,36 @@ def tile_clawmatrix_pa_kernel(
         regroup_tokens(3)
 
         neg_sharpness = const.tile([P, 1], F32)
-        claw_cols = c_psum.tile([P, P], F32)
+        claw_ps = {}
 
         def add_claw_block(piece):
+            if piece == 0:
+                claw_cols = c_psum.tile([P, P], F32, tag="side")
+                claw_ps["cols"] = claw_cols
             for k in range(piece * (BANK // P), (piece + 1) * (BANK // P)):
                 nc.tensor.matmul(
-                    out=claw_cols[:], lhsT=ones_bf16[:], rhs=claw_sb[:, k * P : (k + 1) * P],
+                    out=claw_ps["cols"][:], lhsT=ones_bf16[:], rhs=claw_sb[:, k * P : (k + 1) * P],
                     start=(k == 0), stop=(k == CLAW_PIECES * (BANK // P) - 1),
                 )
 
+        claw_sum = const.tile([P, 1], F32)
+
+        def sum_claw():
+            nc.vector.reduce_sum(out=claw_sum[:], in_=claw_ps["cols"][:], axis=AX.X)
+
         def finish_claw():
-            claw_sum = const.tile([P, 1], F32)
-            nc.vector.reduce_sum(out=claw_sum[:], in_=claw_cols[:], axis=AX.X)
             nc.vector.tensor_scalar_mul(
                 out=neg_sharpness[:], in0=claw_sum[:], scalar1=-1.0 / (D * D * TEMPERATURE)
             )
 
         PAIRS = [(2 * q, 2 * q + 1) for q in range(7)]
-        vis_blocks = [(0, 0), (1, 0), (0, 1), (1, 1)]
-        VIS_STEP = {1: 0, 2: 1, 3: 2, 5: 3}
-        VIS_ENG = ["vector", "scalar", "vector", "scalar"]
-
         def at(t, lag):
             q, g = divmod(t - lag, 2)
             return (PAIRS[q], g) if 0 <= q < len(PAIRS) else None
 
-        pending_w = []
+        vector_piece, tensor_piece, copied_piece = [], [], []
+        V_PIECES = {1: (0, 0), 2: (0, 1), 3: (1, 0), 4: (1, 1)}
+        T_PIECES = {1: (0, 2), 2: (0, 3), 3: (1, 2), 4: (1, 3)}
         for t in range(N_TILES):
             if t >= 1:
                 squared_deviations(t - 1)
@@ -501,11 +546,12 @@ def tile_clawmatrix_pa_kernel(
             if before:
                 gain_and_shift(before[0], 2 * before[1] + 1)
             tok = t + AHEAD - 1
-            tok_engine = "scalar" if t < 3 or tok % 3 else "vector"
+            tok_engine = "scalar" if tok % 4 else "vector"
+            tensor_before = tensor_piece
+            for w in tensor_before:
+                copy_piece(VIS, *w)
             if t >= 1 and tok < N_TILES and tok_engine == "scalar":
                 regroup_tokens(tok)
-            if t >= 2:
-                offset(t - 2)
             if t > 1:
                 add_bias(t, 0)
             add_bias(t, 1)
@@ -514,26 +560,37 @@ def tile_clawmatrix_pa_kernel(
             feat = at(t, 5)
             if feat:
                 regroup_features(*feat)
-            minus_mean(t)
+                minus_mean(t)
             if t >= 1 and tok < N_TILES and tok_engine == "vector":
                 regroup_tokens(tok, "vector")
             if t + 2 < N_TILES:
                 quantise_tokens(t + 2)
+            if not feat:
+                minus_mean(t)
+            if t >= 1 and not V_PIECES.get(t):
+                offset(t - 1)
             if feat:
                 quantise_features(*feat)
-            for w in pending_w:
-                quantise_weights(VIS, *w)
-            pending_w = []
-            if t in VIS_STEP:
-                k = VIS_STEP[t]
-                regroup_weights(VIS, vis_blocks[k][0], vis_blocks[k][1], VIS_ENG[k])
-                pending_w.append(vis_blocks[k])
+            for w in vector_piece:
+                quantise_piece(VIS, *w)
+            for w in copied_piece:
+                quantise_piece(VIS, *w)
+            copied_piece = tensor_before
+            vector_piece = [w for w in [V_PIECES.get(t)] if w]
+            for w in vector_piece:
+                regroup_piece(VIS, w[0], w[1], "vector")
+                offset(t - 1)
             claw_piece = 2 * (t - CLAW_STEP)
             if claw_piece == CLAW_PIECES:
+                sum_claw()
+            if claw_piece == CLAW_PIECES + 2:
                 finish_claw()
             if 1 <= t and t + 1 < N_TILES:
                 project(t + 1, 0)
                 project(t + 1, 1)
+            tensor_piece = [w for w in [T_PIECES.get(t)] if w]
+            for w in tensor_piece:
+                interleave_piece(VIS, *w)
             if 0 <= claw_piece < CLAW_PIECES:
                 add_claw_block(claw_piece)
                 add_claw_block(claw_piece + 1)
@@ -543,8 +600,6 @@ def tile_clawmatrix_pa_kernel(
                 transpose_features(now[0], 2 * now[1] + 1)
             if t + AHEAD < N_TILES:
                 transpose_tokens(t + AHEAD)
-            if t == 5:
-                spread_bias(VIS)
         T14, T15 = (14,), (15,)
         P5, P6 = (10, 11), (12, 13)
         squared_deviations(15)
@@ -563,7 +618,7 @@ def tile_clawmatrix_pa_kernel(
         gain_and_shift(P6, 3)
         normalise_now(15, nc.vector)
         gain_and_shift(T14, 0)
-        gain_and_shift(T14, 1, "vector")
+        gain_and_shift(T14, 1)
         regroup_features(P6, 0)
         similarity(0, 1)
         transpose_features(T15, 0)

@@ -23,7 +23,7 @@ TEMPERATURE = 0.07
 PASSES = D // K_PASS
 HALVES = D // BANK
 CHUNKS = D // P
-RUN = 4
+RUN = 8
 
 LANG, VIS = 0, 1
 UNITS = [(LANG, 0), (LANG, 1), (VIS, 0), (VIS, 1)]

@@ -493,6 +493,9 @@ def tile_clawmatrix_pa_kernel(
         transpose_tokens(2)
         regroup_tokens(2)
         transpose_tokens(3)
+        regroup_tokens(3)
+        transpose_tokens(4)
+        regroup_tokens(4)
         add_bias(0, 0)
         quantise_weights(LANG, 0, 1)
         quantise_tokens(1)
@@ -502,7 +505,6 @@ def tile_clawmatrix_pa_kernel(
         add_bias(1, 0)
         project(1, 1)
         spread_affine()
-        regroup_tokens(3)
 
         neg_sharpness = const.tile([P, 1], F32)
         claw_ps = {}
@@ -546,11 +548,11 @@ def tile_clawmatrix_pa_kernel(
             if before:
                 gain_and_shift(before[0], 2 * before[1] + 1)
             tok = t + AHEAD - 1
-            tok_engine = "scalar" if tok % 4 else "vector"
+            tok_engine = "scalar" if t < 6 or tok % 3 else "vector"
             tensor_before = tensor_piece
             for w in tensor_before:
                 copy_piece(VIS, *w)
-            if t >= 1 and tok < N_TILES and tok_engine == "scalar":
+            if tok > 4 and tok < N_TILES and tok_engine == "scalar":
                 regroup_tokens(tok)
             if t > 1:
                 add_bias(t, 0)
@@ -561,7 +563,7 @@ def tile_clawmatrix_pa_kernel(
             if feat:
                 regroup_features(*feat)
                 minus_mean(t)
-            if t >= 1 and tok < N_TILES and tok_engine == "vector":
+            if tok > 4 and tok < N_TILES and tok_engine == "vector":
                 regroup_tokens(tok, "vector")
             if t + 2 < N_TILES:
                 quantise_tokens(t + 2)
@@ -598,7 +600,7 @@ def tile_clawmatrix_pa_kernel(
             if now:
                 transpose_features(now[0], 2 * now[1])
                 transpose_features(now[0], 2 * now[1] + 1)
-            if t + AHEAD < N_TILES:
+            if 4 < t + AHEAD < N_TILES:
                 transpose_tokens(t + AHEAD)
         T14, T15 = (14,), (15,)
         P5, P6 = (10, 11), (12, 13)

@@ -24,19 +24,19 @@ PASSES = D // K_PASS
 HALVES = D // BANK
 CHUNKS = D // P
 RUN = 8
+PIECE = BANK // 2
+PIECES = D // PIECE
 
 LANG, VIS = 0, 1
 UNITS = [(LANG, 0), (LANG, 1), (VIS, 0), (VIS, 1)]
 TILES_PER_UNIT = TOKENS // P
 N_TILES = len(UNITS) * TILES_PER_UNIT
-GROUP_TILES = 2
-GROUP_TOKENS = GROUP_TILES * P
-N_GROUPS = N_TILES // GROUP_TILES
-GROUPS_PER_UNIT = TILES_PER_UNIT // GROUP_TILES
-CHUNKS_PER_BANK = BANK // GROUP_TOKENS
-BANKS_PER_PASS = PACK // CHUNKS_PER_BANK
+LAST = N_TILES - 1
+PAIRS = [(i, i + 1) for i in range(0, N_TILES - 2, 2)]
+HEAD_TILES = 5
 AHEAD = 4
-CLAW_PIECES = D * D // P // BANK
+CLAW_BLOCKS = D * D // P // P
+CLAW_PER_STEP = CLAW_BLOCKS // 8
 CLAW_STEP = 6
 
 FLOPS = 2 * 2 * BATCHES * TOKENS * D * D + 2 * BATCHES * TOKENS * TOKENS * D
@@ -96,9 +96,9 @@ def tile_clawmatrix_pa_kernel(
                 first = g * K_PASS + u * 2 * P
                 nc.sync.dma_start(
                     out=tile[:, 2 * u : 2 * u + 2, :],
-                    in_=weights[s][first : first + 2 * P, half * BANK : (half + 1) * BANK].rearrange(
-                        "(q e) d -> q e d", e=2
-                    ),
+                    in_=weights[s][
+                        first : first + 2 * P, half * BANK : (half + 1) * BANK
+                    ].rearrange("(q e) d -> q e d", e=2),
                 )
 
         def load_weights(s, g):
@@ -145,7 +145,9 @@ def tile_clawmatrix_pa_kernel(
         zero = const.tile([P, 1], F32)
         nc.vector.memset(zero[:], 0.0)
         eps = const.tile([P, 1], F32)
-        nc.vector.tensor_scalar(out=eps[:], in0=zero[:], scalar1=1.0, scalar2=EPS, op0=ALU.mult, op1=ALU.add)
+        nc.vector.tensor_scalar(
+            out=eps[:], in0=zero[:], scalar1=1.0, scalar2=EPS, op0=ALU.mult, op1=ALU.add
+        )
         ones_bf16 = const.tile([P, P], BF16)
         nc.vector.memset(ones_bf16[:], 1.0)
         ident_f32 = const.tile([P, P], F32)
@@ -177,51 +179,50 @@ def tile_clawmatrix_pa_kernel(
                 nc.scalar.copy(out=dst, in_=src)
             w_grouped[(s, g, half)] = grouped
 
-        PIECE = BANK // 2
-
-        def regroup_piece(s, g, k, engine):
-            grouped = w_grouped_pool.tile([P, PIECE, PACK], BF16, tag="w_piece", align_bytes=64)
-            half, first = divmod(k * PIECE, BANK)
-            dst = grouped[:].rearrange("p (c i) t -> p c t i", i=RUN)
-            src = w_rows[(s, g, half)][:, :, first : first + PIECE].rearrange("p t (c i) -> p c t i", i=RUN)
-            if engine == "vector":
-                nc.vector.tensor_copy(out=dst, in_=src)
-            else:
-                nc.scalar.copy(out=dst, in_=src)
-            w_grouped[(s, g, k, "piece")] = grouped
-
-        w_in_psum = {}
-
-        def interleave_piece(s, g, k):
-            spread = c_psum.tile([P, PIECE, PACK], BF16, tag="side")
-            for part in range(PIECE // P):
-                half, first = divmod(k * PIECE + part * P, BANK)
-                nc.tensor.matmul(
-                    out=spread[:, part * P : (part + 1) * P, :], lhsT=ident_bf16[:],
-                    rhs=w_rows[(s, g, half)][:, :, first : first + P].rearrange("p t d -> p d t"),
-                    start=True, stop=True,
-                )
-            w_in_psum[(s, g, k)] = spread
-
-        def copy_piece(s, g, k):
-            grouped = w_grouped_pool.tile([P, PIECE, PACK], BF16, tag="w_piece", align_bytes=64)
-            nc.scalar.copy(out=grouped[:], in_=w_in_psum[(s, g, k)][:])
-            w_grouped[(s, g, k, "piece")] = grouped
-
-        def quantise_piece(s, g, k):
-            cols = slice(k * PIECE, (k + 1) * PIECE)
-            nc.vector.quantize_mx(
-                out=w_codes[s][:, g, cols].bitcast(FP8X4),
-                scales=w_scales[s][:, g, cols],
-                in_=w_grouped[(s, g, k, "piece")][:].rearrange("p d t -> p (d t)"),
-            )
-
         def quantise_weights(s, g, half):
             cols = slice(half * BANK, (half + 1) * BANK)
             nc.vector.quantize_mx(
                 out=w_codes[s][:, g, cols].bitcast(FP8X4),
                 scales=w_scales[s][:, g, cols],
                 in_=w_grouped[(s, g, half)][:].rearrange("p d t -> p (d t)"),
+            )
+
+        w_pieces = {}
+        w_in_psum = {}
+
+        def piece_rows(g, k, first, width):
+            half, col = divmod(k * PIECE + first, BANK)
+            return w_rows[(VIS, g, half)][:, :, col : col + width]
+
+        def regroup_piece(g, k):
+            grouped = w_grouped_pool.tile([P, PIECE, PACK], BF16, tag="w_piece", align_bytes=64)
+            nc.vector.tensor_copy(
+                out=grouped[:].rearrange("p (c i) t -> p c t i", i=RUN),
+                in_=piece_rows(g, k, 0, PIECE).rearrange("p t (c i) -> p c t i", i=RUN),
+            )
+            w_pieces[(g, k)] = grouped
+
+        def interleave_piece(g, k):
+            spread = c_psum.tile([P, PIECE, PACK], BF16, tag="side")
+            for first in range(0, PIECE, P):
+                nc.tensor.matmul(
+                    out=spread[:, first : first + P, :], lhsT=ident_bf16[:],
+                    rhs=piece_rows(g, k, first, P).rearrange("p t d -> p d t"),
+                    start=True, stop=True,
+                )
+            w_in_psum[(g, k)] = spread
+
+        def copy_piece(g, k):
+            grouped = w_grouped_pool.tile([P, PIECE, PACK], BF16, tag="w_piece", align_bytes=64)
+            nc.scalar.copy(out=grouped[:], in_=w_in_psum[(g, k)][:])
+            w_pieces[(g, k)] = grouped
+
+        def quantise_piece(g, k):
+            cols = slice(k * PIECE, (k + 1) * PIECE)
+            nc.vector.quantize_mx(
+                out=w_codes[VIS][:, g, cols].bitcast(FP8X4),
+                scales=w_scales[VIS][:, g, cols],
+                in_=w_pieces[(g, k)][:].rearrange("p d t -> p (d t)"),
             )
 
         x_grouped, x_quantised, x_transposed = {}, {}, {}
@@ -318,7 +319,8 @@ def tile_clawmatrix_pa_kernel(
         def inverse_deviation(i):
             rstd = stat_pool.tile([P, 1], F32, tag="rstd")
             nc.scalar.activation(
-                out=rstd[:], in_=ssqs[i][:], func=ACT.Abs_reciprocal_sqrt, scale=1.0 / D, bias=eps[:]
+                out=rstd[:], in_=ssqs[i][:], func=ACT.Abs_reciprocal_sqrt, scale=1.0 / D,
+                bias=eps[:],
             )
             rstds[i] = rstd
 
@@ -327,14 +329,14 @@ def tile_clawmatrix_pa_kernel(
             nc.vector.tensor_tensor(out=off[:], in0=neg_means[i][:], in1=rstds[i][:], op=ALU.mult)
             offsets[i] = off
 
-        def normalise(i, engine):
-            engine.tensor_scalar(
+        def normalise_beside_bias_adds(i):
+            nc.gpsimd.tensor_scalar(
                 out=rows[i][:], in0=rows[i][:], scalar1=rstds[i][:], scalar2=offsets[i][:],
                 op0=ALU.mult, op1=ALU.add,
             )
 
-        def normalise_now(i, engine):
-            engine.tensor_scalar(
+        def normalise_at_once(i):
+            nc.vector.tensor_scalar(
                 out=rows[i][:], in0=rows[i][:], scalar1=neg_means[i][:], scalar2=rstds[i][:],
                 op0=ALU.add, op1=ALU.mult,
             )
@@ -354,7 +356,7 @@ def tile_clawmatrix_pa_kernel(
                     )
             row_banks[(tiles, bank)] = yT
 
-        def gain_and_shift(tiles, bank, engine="scalar"):
+        def gain_and_shift(tiles, bank):
             s = UNITS[tiles[0] // TILES_PER_UNIT][0]
             chunks = BANK // (len(tiles) * P)
             g = bank * chunks // PACK
@@ -365,27 +367,21 @@ def tile_clawmatrix_pa_kernel(
                 chunk = bank * chunks + c
                 gain = affine[:, 2 * s * CHUNKS + chunk : 2 * s * CHUNKS + chunk + 1]
                 shift = affine[:, (2 * s + 1) * CHUNKS + chunk : (2 * s + 1) * CHUNKS + chunk + 1]
-                if engine == "scalar":
-                    nc.scalar.activation(
-                        out=acts[(tiles, g)][:, chunk % PACK, :], in_=row_banks[(tiles, bank)][:, c, :],
-                        func=ACT.Identity, scale=gain, bias=shift,
-                    )
-                else:
-                    nc.vector.tensor_scalar(
-                        out=acts[(tiles, g)][:, chunk % PACK, :], in0=row_banks[(tiles, bank)][:, c, :],
-                        scalar1=gain, scalar2=shift, op0=ALU.mult, op1=ALU.add,
-                    )
+                nc.scalar.activation(
+                    out=acts[(tiles, g)][:, chunk % PACK, :],
+                    in_=row_banks[(tiles, bank)][:, c, :],
+                    func=ACT.Identity, scale=gain, bias=shift,
+                )
 
-        def regroup_features(tiles, g, engine="vector"):
+        def regroup_features(tiles, g):
             grouped = grouped_pool.tile(
                 [P, len(tiles) * P, PACK], BF16, tag="grouped", align_bytes=64
             )
-            dst = grouped[:].rearrange("p (c i) j -> p c j i", i=RUN)
-            src = acts[(tiles, g)][:].rearrange("p j (c i) -> p c j i", i=RUN)
-            if engine == "vector":
-                nc.vector.tensor_scalar_max(out=dst, in0=src, scalar1=0.0)
-            else:
-                nc.scalar.activation(out=dst, in_=src, func=ACT.Relu)
+            nc.vector.tensor_scalar_max(
+                out=grouped[:].rearrange("p (c i) j -> p c j i", i=RUN),
+                in0=acts[(tiles, g)][:].rearrange("p j (c i) -> p c j i", i=RUN),
+                scalar1=0.0,
+            )
             grouped_acts[(tiles, g)] = grouped
 
         def quantise_features(tiles, g):
@@ -397,11 +393,11 @@ def tile_clawmatrix_pa_kernel(
                 in_=grouped_acts[(tiles, g)][:].rearrange("p t j -> p (t j)"),
             )
 
-        sims, probs, neg_tops, totals = {}, {}, {}, {}
+        sims, probs, neg_tops, totals, inv_totals = {}, {}, {}, {}, {}
 
-        def similarity(b, n, pool="h"):
+        def similarity(b, n):
             lang_u, vis_u = b, BATCHES + b
-            if pool == "h":
+            if b == 0:
                 sim = h_psum.tile([P, TOKENS], F32, tag="acc")
             else:
                 sim = t_psum.tile([P, TOKENS], F32, tag="transposed")
@@ -436,8 +432,6 @@ def tile_clawmatrix_pa_kernel(
             )
             totals[(b, n)] = total
 
-        inv_totals = {}
-
         def invert_total(b, n):
             inv_total = stat_pool.tile([P, 1], F32, tag="inv_total")
             nc.vector.reciprocal(out=inv_total[:], in_=totals[(b, n)][:])
@@ -450,13 +444,11 @@ def tile_clawmatrix_pa_kernel(
                 nc.vector.tensor_scalar(
                     out=prob[:], in0=prob[:], scalar1=inv_total[:], scalar2=None, op0=ALU.mult
                 )
-            elif engine == "gpsimd":
+            else:
                 nc.gpsimd.tensor_scalar(
                     out=prob[:], in0=prob[:], scalar1=inv_total[:], scalar2=0.0,
                     op0=ALU.mult, op1=ALU.add,
                 )
-            else:
-                nc.scalar.activation(out=prob[:], in_=prob[:], func=ACT.Copy, scale=inv_total[:])
             first = b * TOKENS + n * P
             nc.sync.dma_start(out=out_rows[first : first + P, :], in_=prob[:])
 
@@ -490,12 +482,9 @@ def tile_clawmatrix_pa_kernel(
         transpose_tokens(1)
         regroup_tokens(1)
         regroup_weights(LANG, 1, 1, "vector")
-        transpose_tokens(2)
-        regroup_tokens(2)
-        transpose_tokens(3)
-        regroup_tokens(3)
-        transpose_tokens(4)
-        regroup_tokens(4)
+        for i in range(2, HEAD_TILES):
+            transpose_tokens(i)
+            regroup_tokens(i)
         add_bias(0, 0)
         quantise_weights(LANG, 0, 1)
         quantise_tokens(1)
@@ -509,15 +498,14 @@ def tile_clawmatrix_pa_kernel(
         neg_sharpness = const.tile([P, 1], F32)
         claw_ps = {}
 
-        def add_claw_block(piece):
-            if piece == 0:
+        def add_claw_block(k):
+            if k == 0:
                 claw_cols = c_psum.tile([P, P], F32, tag="side")
                 claw_ps["cols"] = claw_cols
-            for k in range(piece * (BANK // P), (piece + 1) * (BANK // P)):
-                nc.tensor.matmul(
-                    out=claw_ps["cols"][:], lhsT=ones_bf16[:], rhs=claw_sb[:, k * P : (k + 1) * P],
-                    start=(k == 0), stop=(k == CLAW_PIECES * (BANK // P) - 1),
-                )
+            nc.tensor.matmul(
+                out=claw_ps["cols"][:], lhsT=ones_bf16[:], rhs=claw_sb[:, k * P : (k + 1) * P],
+                start=(k == 0), stop=(k == CLAW_BLOCKS - 1),
+            )
 
         claw_sum = const.tile([P, 1], F32)
 
@@ -529,133 +517,134 @@ def tile_clawmatrix_pa_kernel(
                 out=neg_sharpness[:], in0=claw_sum[:], scalar1=-1.0 / (D * D * TEMPERATURE)
             )
 
-        PAIRS = [(2 * q, 2 * q + 1) for q in range(7)]
-        def at(t, lag):
-            q, g = divmod(t - lag, 2)
+        def pair_pass(t, lag):
+            q, g = divmod(t - lag, PASSES)
             return (PAIRS[q], g) if 0 <= q < len(PAIRS) else None
 
-        vector_piece, tensor_piece, copied_piece = [], [], []
-        V_PIECES = {1: (0, 0), 2: (0, 1), 3: (1, 0), 4: (1, 1)}
-        T_PIECES = {1: (0, 2), 2: (0, 3), 3: (1, 2), 4: (1, 3)}
+        def vision_piece(t):
+            return divmod(t - 1, PIECES // 2) if 1 <= t <= PASSES * PIECES // 2 else None
+
         for t in range(N_TILES):
+            before = pair_pass(t, 4)
             if t >= 1:
                 squared_deviations(t - 1)
-            before = at(t, 4)
             if before:
                 gain_and_shift(before[0], 2 * before[1])
             if t >= 1:
                 inverse_deviation(t - 1)
             if before:
                 gain_and_shift(before[0], 2 * before[1] + 1)
+            last_piece = vision_piece(t - 1)
+            if last_piece:
+                copy_piece(last_piece[0], last_piece[1] + PIECES // 2)
             tok = t + AHEAD - 1
             tok_engine = "scalar" if t < 6 or tok % 3 else "vector"
-            tensor_before = tensor_piece
-            for w in tensor_before:
-                copy_piece(VIS, *w)
-            if tok > 4 and tok < N_TILES and tok_engine == "scalar":
+            to_copy = HEAD_TILES <= tok < N_TILES
+            if to_copy and tok_engine == "scalar":
                 regroup_tokens(tok)
+
             if t > 1:
                 add_bias(t, 0)
             add_bias(t, 1)
             if t >= 2:
-                normalise(t - 2, nc.gpsimd)
-            feat = at(t, 5)
+                normalise_beside_bias_adds(t - 2)
+            feat = pair_pass(t, 5)
             if feat:
                 regroup_features(*feat)
                 minus_mean(t)
-            if tok > 4 and tok < N_TILES and tok_engine == "vector":
+            if to_copy and tok_engine == "vector":
                 regroup_tokens(tok, "vector")
             if t + 2 < N_TILES:
                 quantise_tokens(t + 2)
             if not feat:
                 minus_mean(t)
-            if t >= 1 and not V_PIECES.get(t):
+            piece = vision_piece(t)
+            if 1 <= t < LAST and not piece:
                 offset(t - 1)
+            if t == LAST:
+                finish_claw()
             if feat:
                 quantise_features(*feat)
-            for w in vector_piece:
-                quantise_piece(VIS, *w)
-            for w in copied_piece:
-                quantise_piece(VIS, *w)
-            copied_piece = tensor_before
-            vector_piece = [w for w in [V_PIECES.get(t)] if w]
-            for w in vector_piece:
-                regroup_piece(VIS, w[0], w[1], "vector")
+            if last_piece:
+                quantise_piece(*last_piece)
+            copied_piece = vision_piece(t - 2)
+            if copied_piece:
+                quantise_piece(copied_piece[0], copied_piece[1] + PIECES // 2)
+            if piece:
+                regroup_piece(*piece)
                 offset(t - 1)
-            claw_piece = 2 * (t - CLAW_STEP)
-            if claw_piece == CLAW_PIECES:
+            claw_block = CLAW_PER_STEP * (t - CLAW_STEP)
+            if claw_block == CLAW_BLOCKS:
                 sum_claw()
-            if claw_piece == CLAW_PIECES + 2:
-                finish_claw()
-            if 1 <= t and t + 1 < N_TILES:
-                project(t + 1, 0)
-                project(t + 1, 1)
-            tensor_piece = [w for w in [T_PIECES.get(t)] if w]
-            for w in tensor_piece:
-                interleave_piece(VIS, *w)
-            if 0 <= claw_piece < CLAW_PIECES:
-                add_claw_block(claw_piece)
-                add_claw_block(claw_piece + 1)
-            now = at(t, 3)
+
+            if 1 <= t < LAST:
+                for half in range(HALVES):
+                    project(t + 1, half)
+            if piece:
+                interleave_piece(piece[0], piece[1] + PIECES // 2)
+            if 0 <= claw_block < CLAW_BLOCKS:
+                for k in range(claw_block, claw_block + CLAW_PER_STEP):
+                    add_claw_block(k)
+            now = pair_pass(t, 3)
             if now:
                 transpose_features(now[0], 2 * now[1])
                 transpose_features(now[0], 2 * now[1] + 1)
-            if 4 < t + AHEAD < N_TILES:
+            if HEAD_TILES <= t + AHEAD < N_TILES:
                 transpose_tokens(t + AHEAD)
-        T14, T15 = (14,), (15,)
-        P5, P6 = (10, 11), (12, 13)
-        squared_deviations(15)
-        inverse_deviation(15)
-        normalise_now(14, nc.vector)
-        gain_and_shift(P6, 0)
-        gain_and_shift(P6, 1)
-        regroup_features(P5, 1)
-        transpose_features(P6, 2)
-        transpose_features(P6, 3)
-        transpose_features(T14, 0)
-        transpose_features(T14, 1)
+
+        last_pair = PAIRS[-1]
+        single, final = (LAST - 1,), (LAST,)
+        squared_deviations(LAST)
+        inverse_deviation(LAST)
+        normalise_at_once(LAST - 1)
         similarity(0, 0)
-        quantise_features(P5, 1)
-        gain_and_shift(P6, 2)
-        gain_and_shift(P6, 3)
-        normalise_now(15, nc.vector)
-        gain_and_shift(T14, 0)
-        gain_and_shift(T14, 1)
-        regroup_features(P6, 0)
-        similarity(0, 1)
-        transpose_features(T15, 0)
-        transpose_features(T15, 1)
-        gain_and_shift(T15, 0)
-        gain_and_shift(T15, 1)
+        gain_and_shift(last_pair, 0)
+        gain_and_shift(last_pair, 1)
+        regroup_features(PAIRS[-2], 1)
         negated_logits(0, 0)
-        quantise_features(P6, 0)
-        regroup_features(P6, 1)
-        negated_logits(0, 1)
-        quantise_features(P6, 1)
-        regroup_features(T14, 1)
-        regroup_features(T14, 0)
+        transpose_features(last_pair, 2)
+        transpose_features(last_pair, 3)
+        for g in range(PASSES):
+            transpose_features(single, g)
+        quantise_features(PAIRS[-2], 1)
+        gain_and_shift(last_pair, 2)
+        gain_and_shift(last_pair, 3)
+        normalise_at_once(LAST)
+        for g in range(PASSES):
+            gain_and_shift(single, g)
+        regroup_features(last_pair, 0)
+        similarity(0, 1)
+        for g in range(PASSES):
+            transpose_features(final, g)
         similarity(0, 2)
+        for g in range(PASSES):
+            gain_and_shift(final, g)
+        negated_logits(0, 1)
+        quantise_features(last_pair, 0)
+        regroup_features(last_pair, 1)
+        negated_logits(0, 2)
+        quantise_features(last_pair, 1)
+        for g in range(PASSES):
+            regroup_features(single, g)
         similarity(0, 3)
         exponentials(0, 0)
         exponentials(0, 1)
-        quantise_features(T14, 1)
-        quantise_features(T14, 0)
-        negated_logits(0, 2)
-        similarity(1, 0, "t")
-        similarity(1, 1, "t")
-        similarity(1, 2, "t")
-        regroup_features(T15, 0)
-        regroup_features(T15, 1)
+        for g in range(PASSES):
+            quantise_features(single, g)
         negated_logits(0, 3)
+        for n in range(TILES_PER_UNIT - 1):
+            similarity(1, n)
+        for g in range(PASSES):
+            regroup_features(final, g)
+        negated_logits(1, 0)
         exponentials(0, 2)
         exponentials(0, 3)
-        quantise_features(T15, 0)
-        quantise_features(T15, 1)
-        similarity(1, 3, "t")
-        invert_total(0, 0)
-        negated_logits(1, 0)
-        invert_total(0, 1)
+        for g in range(PASSES):
+            quantise_features(final, g)
+        similarity(1, 3)
         negated_logits(1, 1)
+        invert_total(0, 0)
+        invert_total(0, 1)
         store_probabilities(0, 0, "gpsimd")
         store_probabilities(0, 1, "gpsimd")
         exponentials(1, 0)
@@ -667,12 +656,9 @@ def tile_clawmatrix_pa_kernel(
         store_probabilities(0, 2, "gpsimd")
         exponentials(1, 2)
         exponentials(1, 3)
-        store_probabilities(0, 3)
         invert_total(1, 0)
-        invert_total(1, 1)
-        store_probabilities(1, 0)
-        store_probabilities(1, 1)
-        invert_total(1, 2)
-        invert_total(1, 3)
-        store_probabilities(1, 2)
-        store_probabilities(1, 3)
+        store_probabilities(0, 3)
+        for n in range(TILES_PER_UNIT - 1):
+            invert_total(1, n + 1)
+            store_probabilities(1, n)
+        store_probabilities(1, TILES_PER_UNIT - 1)

@@ -597,15 +597,14 @@ def tile_clawmatrix_pa_kernel(
         squared_deviations(LAST)
         inverse_deviation(LAST)
         normalise_at_once(LAST - 1)
-        similarity(0, 0)
         gain_and_shift(last_pair, 0)
         gain_and_shift(last_pair, 1)
         regroup_features(PAIRS[-2], 1)
-        negated_logits(0, 0)
         transpose_features(last_pair, 2)
         transpose_features(last_pair, 3)
         for g in range(PASSES):
             transpose_features(single, g)
+        similarity(0, 0)
         quantise_features(PAIRS[-2], 1)
         gain_and_shift(last_pair, 2)
         gain_and_shift(last_pair, 3)
@@ -616,35 +615,36 @@ def tile_clawmatrix_pa_kernel(
         similarity(0, 1)
         for g in range(PASSES):
             transpose_features(final, g)
-        similarity(0, 2)
         for g in range(PASSES):
             gain_and_shift(final, g)
-        negated_logits(0, 1)
+        negated_logits(0, 0)
         quantise_features(last_pair, 0)
         regroup_features(last_pair, 1)
-        negated_logits(0, 2)
+        negated_logits(0, 1)
         quantise_features(last_pair, 1)
         for g in range(PASSES):
             regroup_features(single, g)
+        similarity(0, 2)
         similarity(0, 3)
         exponentials(0, 0)
         exponentials(0, 1)
         for g in range(PASSES):
             quantise_features(single, g)
-        negated_logits(0, 3)
+        negated_logits(0, 2)
         for n in range(TILES_PER_UNIT - 1):
             similarity(1, n)
         for g in range(PASSES):
             regroup_features(final, g)
-        negated_logits(1, 0)
+        negated_logits(0, 3)
         exponentials(0, 2)
         exponentials(0, 3)
         for g in range(PASSES):
             quantise_features(final, g)
         similarity(1, 3)
-        negated_logits(1, 1)
         invert_total(0, 0)
+        negated_logits(1, 0)
         invert_total(0, 1)
+        negated_logits(1, 1)
         store_probabilities(0, 0, "gpsimd")
         store_probabilities(0, 1, "gpsimd")
         exponentials(1, 0)

from contextlib import ExitStack

import concourse.mybir as mybir
from concourse.masks import make_identity

F32 = mybir.dt.float32
BF16 = mybir.dt.bfloat16
U32 = mybir.dt.uint32
U8 = mybir.dt.uint8
FP8X4 = mybir.dt.float8_e4m3fn_x4
ALU = mybir.AluOpType
ACT = mybir.ActivationFunctionType
AX = mybir.AxisListType

P = 128
PACK = 4
K_PASS = P * PACK
BANK = 512

BATCHES, TOKENS, D = 2, 512, 1024
EPS = 1e-5
TEMPERATURE = 0.07
PASSES = D // K_PASS
HALVES = D // BANK
CHUNKS = D // P
RUN = 8
PIECE = BANK // 2
PIECES = D // PIECE

LANG, VIS = 0, 1
UNITS = [(LANG, 0), (LANG, 1), (VIS, 0), (VIS, 1)]
TILES_PER_UNIT = TOKENS // P
N_TILES = len(UNITS) * TILES_PER_UNIT
LAST = N_TILES - 1
PAIRS = [(i, i + 1) for i in range(0, N_TILES - 2, 2)]
HEAD_TILES = 5
AHEAD = 4
CLAW_BLOCKS = D * D // P // P
CLAW_PER_STEP = CLAW_BLOCKS // 8
CLAW_STEP = 6

FLOPS = 2 * 2 * BATCHES * TOKENS * D * D + 2 * BATCHES * TOKENS * TOKENS * D


def tile_clawmatrix_pa_kernel(
    tc, vision_features, language_features, vW, vb, vg, vbeta, lW, lb, lg, lbeta, claw, out
):
    nc = tc.nc
    features = (language_features.flatten_outer_dims(), vision_features.flatten_outer_dims())
    weights = (lW, vW)
    biases = (lb, vb)
    gains = (lg, vg)
    shifts = (lbeta, vbeta)
    out_rows = out.flatten_outer_dims()

    with ExitStack() as ctx:
        const = ctx.enter_context(tc.tile_pool(name="const", bufs=1))
        resident = ctx.enter_context(tc.tile_pool(name="resident", bufs=1))
        w_grouped_pool = ctx.enter_context(tc.tile_pool(name="w_grouped", bufs=3))
        grouped_pool = ctx.enter_context(tc.tile_pool(name="grouped", bufs=5))
        token_pool = ctx.enter_context(tc.tile_pool(name="tokens", bufs=AHEAD + 2))
        row_pool = ctx.enter_context(tc.tile_pool(name="rows", bufs=7))
        scrap_pool = ctx.enter_context(tc.tile_pool(name="scrap", bufs=1))
        act_pool = ctx.enter_context(tc.tile_pool(name="act", bufs=6))
        prob_pool = ctx.enter_context(tc.tile_pool(name="probs", bufs=BATCHES * TILES_PER_UNIT))
        stat_pool = ctx.enter_context(tc.tile_pool(name="stats", bufs=8))
        h_psum = ctx.enter_context(tc.psum_pool(name="h_psum", bufs=HALVES))
        t_psum = ctx.enter_context(tc.psum_pool(name="t_psum", bufs=5))
        c_psum = ctx.enter_context(tc.psum_pool(name="c_psum", bufs=1))
        ctx.enter_context(tc.manual_schedule())

        bias_rows = const.tile([P, D], BF16)
        nc.vector.memset(bias_rows[:].bitcast(U32), 0)
        bias_tiles = [
            const.tile([P, D], BF16, name="bias_lang"),
            const.tile([P, D], BF16, name="bias_vis"),
        ]
        affine_rows = const.tile([P, P], BF16)
        nc.vector.memset(affine_rows[:].bitcast(U32), 0)

        x_tiles = []

        def load_tokens(i):
            s, b = UNITS[i // TILES_PER_UNIT]
            first = b * TOKENS + (i % TILES_PER_UNIT) * P
            x_tile = resident.tile([P, D], BF16, name="x_tile%d" % i)
            nc.sync.dma_start(out=x_tile[:], in_=features[s][first : first + P, :])
            x_tiles.append(x_tile)

        w_rows = {}

        def load_weights_by_halves(s, g, half):
            tile = resident.tile([P, PACK, BANK], BF16, name="w_rows%d_%d_%d" % (s, g, half))
            w_rows[(s, g, half)] = tile[:]
            for u in range(2):
                first = g * K_PASS + u * 2 * P
                nc.sync.dma_start(
                    out=tile[:, 2 * u : 2 * u + 2, :],
                    in_=weights[s][
                        first : first + 2 * P, half * BANK : (half + 1) * BANK
                    ].rearrange("(q e) d -> q e d", e=2),
                )

        def load_weights(s, g):
            tile = resident.tile([P, PACK, D], BF16, name="w_rows%d_%d" % (s, g))
            nc.sync.dma_start(
                out=tile[:].rearrange("q (u e) d -> q u e d", u=2),
                in_=weights[s][g * K_PASS : (g + 1) * K_PASS, :].rearrange(
                    "(u q e) d -> q u e d", u=2, e=2
                ),
            )
            for half in range(HALVES):
                w_rows[(s, g, half)] = tile[:, :, half * BANK : (half + 1) * BANK]

        for half in range(HALVES):
            for g in range(PASSES):
                load_weights_by_halves(LANG, g, half)
            if half == 0:
                load_tokens(0)
                nc.sync.dma_start(
                    out=bias_rows[0:1, :], in_=biases[LANG].rearrange("(o d) -> o d", o=1)
                )
        for i in range(1, 4):
            load_tokens(i)
        for s in (LANG, VIS):
            for v, vector in enumerate((gains[s], shifts[s])):
                first = (2 * s + v) * CHUNKS
                nc.sync.dma_start(
                    out=affine_rows[first : first + CHUNKS, :],
                    in_=vector.rearrange("(c p) -> c p", p=P),
                )
        for i in range(4, 8):
            load_tokens(i)
        for g in range(PASSES):
            load_weights(VIS, g)
        for i in range(8, N_TILES):
            load_tokens(i)
        nc.sync.dma_start(out=bias_tiles[VIS][:], in_=biases[VIS].partition_broadcast(P))
        claw_sb = resident.tile([P, D * D // P], BF16)
        nc.sync.dma_start(out=claw_sb[:], in_=claw.rearrange("(p r) c -> p (r c)", p=P))

        warm = const.tile([P, 1], F32)
        nc.vector.memset(warm[:], 1.0)
        nc.scalar.activation(out=warm[:], in_=warm[:], func=ACT.Abs_reciprocal_sqrt)
        zero = const.tile([P, 1], F32)
        nc.vector.memset(zero[:], 0.0)
        eps = const.tile([P, 1], F32)
        nc.vector.tensor_scalar(
            out=eps[:], in0=zero[:], scalar1=1.0, scalar2=EPS, op0=ALU.mult, op1=ALU.add
        )
        ones_bf16 = const.tile([P, P], BF16)
        nc.vector.memset(ones_bf16[:], 1.0)
        ident_f32 = const.tile([P, P], F32)
        make_identity(nc, ident_f32[:])
        ident_bf16 = const.tile([P, P], BF16)
        nc.vector.tensor_copy(out=ident_bf16[:], in_=ident_f32[:])

        w_codes, w_scales, a_codes, a_scales = [], [], [], []
        for s in (LANG, VIS):
            wc = resident.tile([P, PASSES, D], U32, name="w_codes%d" % s, align_bytes=64)
            ws = resident.tile([P, PASSES, D], U8, name="w_scales%d" % s, align_bytes=64)
            w_codes.append(wc)
            w_scales.append(ws)
        for u in range(len(UNITS)):
            ac = resident.tile([P, PASSES, TOKENS], U32, name="a_codes%d" % u, align_bytes=64)
            asc = resident.tile([P, PASSES, TOKENS], U8, name="a_scales%d" % u, align_bytes=64)
            a_codes.append(ac)
            a_scales.append(asc)

        w_grouped = {}

        def regroup_weights(s, g, half, engine):
            grouped = w_grouped_pool.tile([P, BANK, PACK], BF16, tag="w_grouped", align_bytes=64)
            dst = grouped[:].rearrange("p (c i) t -> p c t i", i=RUN)
            src = w_rows[(s, g, half)].rearrange("p t (c i) -> p c t i", i=RUN)
            if engine == "vector":
                nc.vector.tensor_copy(out=dst, in_=src)
            else:
                nc.scalar.copy(out=dst, in_=src)
            w_grouped[(s, g, half)] = grouped

        def quantise_weights(s, g, half):
            cols = slice(half * BANK, (half + 1) * BANK)
            nc.vector.quantize_mx(
                out=w_codes[s][:, g, cols].bitcast(FP8X4),
                scales=w_scales[s][:, g, cols],
                in_=w_grouped[(s, g, half)][:].rearrange("p d t -> p (d t)"),
            )

        w_pieces = {}
        w_in_psum = {}

        def piece_rows(g, k, first, width):
            half, col = divmod(k * PIECE + first, BANK)
            return w_rows[(VIS, g, half)][:, :, col : col + width]

        def regroup_piece(g, k):
            grouped = w_grouped_pool.tile([P, PIECE, PACK], BF16, tag="w_piece", align_bytes=64)
            nc.vector.tensor_copy(
                out=grouped[:].rearrange("p (c i) t -> p c t i", i=RUN),
                in_=piece_rows(g, k, 0, PIECE).rearrange("p t (c i) -> p c t i", i=RUN),
            )
            w_pieces[(g, k)] = grouped

        def interleave_piece(g, k):
            spread = c_psum.tile([P, PIECE, PACK], BF16, tag="side")
            for first in range(0, PIECE, P):
                nc.tensor.matmul(
                    out=spread[:, first : first + P, :], lhsT=ident_bf16[:],
                    rhs=piece_rows(g, k, first, P).rearrange("p t d -> p d t"),
                    start=True, stop=True,
                )
            w_in_psum[(g, k)] = spread

        def copy_piece(g, k):
            grouped = w_grouped_pool.tile([P, PIECE, PACK], BF16, tag="w_piece", align_bytes=64)
            nc.scalar.copy(out=grouped[:], in_=w_in_psum[(g, k)][:])
            w_pieces[(g, k)] = grouped

        def quantise_piece(g, k):
            cols = slice(k * PIECE, (k + 1) * PIECE)
            nc.vector.quantize_mx(
                out=w_codes[VIS][:, g, cols].bitcast(FP8X4),
                scales=w_scales[VIS][:, g, cols],
                in_=w_pieces[(g, k)][:].rearrange("p d t -> p (d t)"),
            )

        x_grouped, x_quantised, x_transposed = {}, {}, {}

        def transpose_tokens(i):
            words = x_tiles[i][:].bitcast(F32)
            xT = t_psum.tile([P, PACK, P], F32, tag="transposed")
            for q in range(PACK):
                nc.tensor.transpose(
                    out=xT[:, q, :], in_=words[:, q * P : (q + 1) * P], identity=ident_f32[:]
                )
            x_transposed[i] = xT

        def regroup_tokens(i, engine="scalar"):
            grouped = token_pool.tile([P, PASSES, P, 2], F32, tag="x_grouped", align_bytes=64)
            src = x_transposed[i][:].rearrange("p (g u) t -> p g t u", u=2)
            if engine == "scalar":
                nc.scalar.copy(out=grouped[:], in_=src)
            else:
                nc.vector.tensor_copy(out=grouped[:], in_=src)
            x_grouped[i] = grouped

        def quantise_tokens(i):
            x_codes = token_pool.tile([P, PASSES * P], U32, tag="x_codes", align_bytes=64)
            x_scales = token_pool.tile([P, PASSES * P], U8, tag="x_scales", align_bytes=64)
            nc.vector.quantize_mx(
                out=x_codes[:].bitcast(FP8X4),
                scales=x_scales[:],
                in_=x_grouped[i][:].rearrange("p g t u -> p (g t u)").bitcast(BF16),
            )
            x_quantised[i] = (x_codes, x_scales)

        projected = {}

        def project(i, half):
            s = UNITS[i // TILES_PER_UNIT][0]
            x_codes, x_scales = x_quantised[i]
            cols = slice(half * BANK, (half + 1) * BANK)
            acc = h_psum.tile([P, BANK], F32, tag="acc")
            for g in range(PASSES):
                toks = slice(g * P, (g + 1) * P)
                nc.tensor.matmul_mx(
                    out=acc[:],
                    lhsT=x_codes[:, toks].bitcast(FP8X4),
                    lhsT_scale=x_scales[:, toks],
                    rhs=w_codes[s][:, g, cols].bitcast(FP8X4),
                    rhs_scale=w_scales[s][:, g, cols],
                    start=(g == 0),
                    stop=(g == PASSES - 1),
                )
            projected[(i, half)] = acc

        rows, sums, neg_means, ssqs, rstds, offsets = {}, {}, {}, {}, {}, {}

        def add_bias(i, half):
            s = UNITS[i // TILES_PER_UNIT][0]
            cols = slice(half * BANK, (half + 1) * BANK)
            if half == 0:
                h = row_pool.tile([P, D], F32, tag="h")
                sums_of_i = stat_pool.tile([P, HALVES], F32, tag="sums")
                rows[i] = h
                sums[i] = sums_of_i
            nc.vector.scalar_tensor_tensor(
                out=rows[i][:, cols],
                in0=projected[(i, half)][:],
                scalar=1.0,
                in1=bias_tiles[s][:, cols],
                op0=ALU.mult,
                op1=ALU.add,
                accum_out=sums[i][:, half : half + 1],
            )

        def minus_mean(i):
            neg_mean = stat_pool.tile([P, 1], F32, tag="neg_mean")
            nc.vector.tensor_scalar(
                out=neg_mean[:],
                in0=sums[i][:, 0:1],
                scalar1=sums[i][:, 1:2],
                scalar2=-1.0 / D,
                op0=ALU.add,
                op1=ALU.mult,
            )
            neg_means[i] = neg_mean

        def squared_deviations(i):
            scrap = scrap_pool.tile([P, D], BF16, tag="scrap")
            ssq = stat_pool.tile([P, 1], F32, tag="ssq")
            nc.scalar.activation(
                out=scrap[:], in_=rows[i][:], func=ACT.Square, bias=neg_means[i][:], scale=1.0,
                accum_out=ssq[:],
            )
            ssqs[i] = ssq

        def inverse_deviation(i):
            rstd = stat_pool.tile([P, 1], F32, tag="rstd")
            nc.scalar.activation(
                out=rstd[:], in_=ssqs[i][:], func=ACT.Abs_reciprocal_sqrt, scale=1.0 / D,
                bias=eps[:],
            )
            rstds[i] = rstd

        def offset(i):
            off = stat_pool.tile([P, 1], F32, tag="offset")
            nc.vector.tensor_tensor(out=off[:], in0=neg_means[i][:], in1=rstds[i][:], op=ALU.mult)
            offsets[i] = off

        def normalise_beside_bias_adds(i):
            nc.gpsimd.tensor_scalar(
                out=rows[i][:], in0=rows[i][:], scalar1=rstds[i][:], scalar2=offsets[i][:],
                op0=ALU.mult, op1=ALU.add,
            )

        def normalise_at_once(i):
            nc.vector.tensor_scalar(
                out=rows[i][:], in0=rows[i][:], scalar1=neg_means[i][:], scalar2=rstds[i][:],
                op0=ALU.add, op1=ALU.mult,
            )

        row_banks, acts, grouped_acts = {}, {}, {}

        def transpose_features(tiles, bank):
            chunks = BANK // (len(tiles) * P)
            yT = t_psum.tile([P, chunks, len(tiles) * P], F32, tag="transposed")
            for c in range(chunks):
                for r, i in enumerate(tiles):
                    first = (bank * chunks + c) * P
                    nc.tensor.transpose(
                        out=yT[:, c, r * P : (r + 1) * P],
                        in_=rows[i][:, first : first + P],
                        identity=ident_f32[:],
                    )
            row_banks[(tiles, bank)] = yT

        def gain_and_shift(tiles, bank):
            s = UNITS[tiles[0] // TILES_PER_UNIT][0]
            chunks = BANK // (len(tiles) * P)
            g = bank * chunks // PACK
            if (tiles, g) not in acts:
                act = act_pool.tile([P, PACK, len(tiles) * P], BF16, tag="act")
                acts[(tiles, g)] = act
            for c in range(chunks):
                chunk = bank * chunks + c
                gain = affine[:, 2 * s * CHUNKS + chunk : 2 * s * CHUNKS + chunk + 1]
                shift = affine[:, (2 * s + 1) * CHUNKS + chunk : (2 * s + 1) * CHUNKS + chunk + 1]
                nc.scalar.activation(
                    out=acts[(tiles, g)][:, chunk % PACK, :],
                    in_=row_banks[(tiles, bank)][:, c, :],
                    func=ACT.Identity, scale=gain, bias=shift,
                )

        def regroup_features(tiles, g):
            grouped = grouped_pool.tile(
                [P, len(tiles) * P, PACK], BF16, tag="grouped", align_bytes=64
            )
            nc.vector.tensor_scalar_max(
                out=grouped[:].rearrange("p (c i) j -> p c j i", i=RUN),
                in0=acts[(tiles, g)][:].rearrange("p j (c i) -> p c j i", i=RUN),
                scalar1=0.0,
            )
            grouped_acts[(tiles, g)] = grouped

        def quantise_features(tiles, g):
            u, first = divmod(tiles[0], TILES_PER_UNIT)
            toks = slice(first * P, (first + len(tiles)) * P)
            nc.vector.quantize_mx(
                out=a_codes[u][:, g, toks].bitcast(FP8X4),
                scales=a_scales[u][:, g, toks],
                in_=grouped_acts[(tiles, g)][:].rearrange("p t j -> p (t j)"),
            )

        sims, probs, neg_tops, totals, inv_totals = {}, {}, {}, {}, {}

        def similarity(b, n):
            lang_u, vis_u = b, BATCHES + b
            if b == 0:
                sim = h_psum.tile([P, TOKENS], F32, tag="acc")
            else:
                sim = t_psum.tile([P, TOKENS], F32, tag="transposed")
            toks = slice(n * P, (n + 1) * P)
            for g in range(PASSES):
                nc.tensor.matmul_mx(
                    out=sim[:],
                    lhsT=a_codes[vis_u][:, g, toks].bitcast(FP8X4),
                    lhsT_scale=a_scales[vis_u][:, g, toks],
                    rhs=a_codes[lang_u][:, g, :].bitcast(FP8X4),
                    rhs_scale=a_scales[lang_u][:, g, :],
                    start=(g == 0),
                    stop=(g == PASSES - 1),
                )
            sims[(b, n)] = sim

        def negated_logits(b, n):
            prob = prob_pool.tile([P, TOKENS], F32, tag="probs")
            neg_top = stat_pool.tile([P, 1], F32, tag="neg_top")
            nc.vector.tensor_scalar(
                out=prob[:], in0=sims[(b, n)][:], scalar1=neg_sharpness[:], scalar2=None,
                op0=ALU.mult, op1=ALU.min, accum_out=neg_top[:],
            )
            probs[(b, n)] = prob
            neg_tops[(b, n)] = neg_top

        def exponentials(b, n):
            total = stat_pool.tile([P, 1], F32, tag="total")
            nc.scalar.activation(
                out=probs[(b, n)][:], in_=probs[(b, n)][:], func=ACT.Exp, bias=neg_tops[(b, n)][:],
                scale=-1.0, accum_out=total[:],
            )
            totals[(b, n)] = total

        def invert_total(b, n):
            inv_total = stat_pool.tile([P, 1], F32, tag="inv_total")
            nc.vector.reciprocal(out=inv_total[:], in_=totals[(b, n)][:])
            inv_totals[(b, n)] = inv_total

        def store_probabilities(b, n, engine="vector"):
            prob = probs[(b, n)]
            inv_total = inv_totals[(b, n)]
            if engine == "vector":
                nc.vector.tensor_scalar(
                    out=prob[:], in0=prob[:], scalar1=inv_total[:], scalar2=None, op0=ALU.mult
                )
            else:
                nc.gpsimd.tensor_scalar(
                    out=prob[:], in0=prob[:], scalar1=inv_total[:], scalar2=0.0,
                    op0=ALU.mult, op1=ALU.add,
                )
            first = b * TOKENS + n * P
            nc.sync.dma_start(out=out_rows[first : first + P, :], in_=prob[:])

        def spread_bias():
            spread = t_psum.tile([P, D], BF16, tag="transposed")
            for half in range(HALVES):
                cols = slice(half * BANK, (half + 1) * BANK)
                nc.tensor.matmul(
                    out=spread[:, cols], lhsT=ones_bf16[:], rhs=bias_rows[:, cols],
                    start=True, stop=True,
                )
            nc.scalar.copy(out=bias_tiles[LANG][:], in_=spread[:])

        affine = const.tile([P, 4 * CHUNKS], F32)

        def spread_affine():
            affine_ps = t_psum.tile([P, P], BF16, tag="transposed")
            nc.tensor.transpose(out=affine_ps[:], in_=affine_rows[:], identity=ident_bf16[:])
            nc.scalar.copy(out=affine[:], in_=affine_ps[:, 0 : 4 * CHUNKS])

        regroup_weights(LANG, 0, 0, "vector")
        regroup_weights(LANG, 1, 0, "vector")
        transpose_tokens(0)
        regroup_tokens(0)
        spread_bias()
        quantise_weights(LANG, 0, 0)
        regroup_weights(LANG, 0, 1, "scalar")
        quantise_tokens(0)
        quantise_weights(LANG, 1, 0)
        project(0, 0)
        transpose_tokens(1)
        regroup_tokens(1)
        regroup_weights(LANG, 1, 1, "vector")
        for i in range(2, HEAD_TILES):
            transpose_tokens(i)
            regroup_tokens(i)
        add_bias(0, 0)
        quantise_weights(LANG, 0, 1)
        quantise_tokens(1)
        quantise_weights(LANG, 1, 1)
        project(1, 0)
        project(0, 1)
        add_bias(1, 0)
        project(1, 1)
        spread_affine()

        neg_sharpness = const.tile([P, 1], F32)
        claw_ps = {}

        def add_claw_block(k):
            if k == 0:
                claw_cols = c_psum.tile([P, P], F32, tag="side")
                claw_ps["cols"] = claw_cols
            nc.tensor.matmul(
                out=claw_ps["cols"][:], lhsT=ones_bf16[:], rhs=claw_sb[:, k * P : (k + 1) * P],
                start=(k == 0), stop=(k == CLAW_BLOCKS - 1),
            )

        claw_sum = const.tile([P, 1], F32)

        def sum_claw():
            nc.vector.reduce_sum(out=claw_sum[:], in_=claw_ps["cols"][:], axis=AX.X)

        def finish_claw():
            nc.vector.tensor_scalar_mul(
                out=neg_sharpness[:], in0=claw_sum[:], scalar1=-1.0 / (D * D * TEMPERATURE)
            )

        def pair_pass(t, lag):
            q, g = divmod(t - lag, PASSES)
            return (PAIRS[q], g) if 0 <= q < len(PAIRS) else None

        def vision_piece(t):
            return divmod(t - 1, PIECES // 2) if 1 <= t <= PASSES * PIECES // 2 else None

        for t in range(N_TILES):
            before = pair_pass(t, 4)
            if t >= 1:
                squared_deviations(t - 1)
            if before:
                gain_and_shift(before[0], 2 * before[1])
            if t >= 1:
                inverse_deviation(t - 1)
            if before:
                gain_and_shift(before[0], 2 * before[1] + 1)
            last_piece = vision_piece(t - 1)
            if last_piece:
                copy_piece(last_piece[0], last_piece[1] + PIECES // 2)
            tok = t + AHEAD - 1
            tok_engine = "scalar" if t < 6 or tok % 3 else "vector"
            to_copy = HEAD_TILES <= tok < N_TILES
            if to_copy and tok_engine == "scalar":
                regroup_tokens(tok)

            if t > 1:
                add_bias(t, 0)
            add_bias(t, 1)
            if t >= 2:
                normalise_beside_bias_adds(t - 2)
            feat = pair_pass(t, 5)
            if feat:
                regroup_features(*feat)
                minus_mean(t)
            if to_copy and tok_engine == "vector":
                regroup_tokens(tok, "vector")
            if t + 2 < N_TILES:
                quantise_tokens(t + 2)
            if not feat:
                minus_mean(t)
            piece = vision_piece(t)
            if 1 <= t < LAST and not piece:
                offset(t - 1)
            if t == LAST:
                finish_claw()
            if feat:
                quantise_features(*feat)
            if last_piece:
                quantise_piece(*last_piece)
            copied_piece = vision_piece(t - 2)
            if copied_piece:
                quantise_piece(copied_piece[0], copied_piece[1] + PIECES // 2)
            if piece:
                regroup_piece(*piece)
                offset(t - 1)
            claw_block = CLAW_PER_STEP * (t - CLAW_STEP)
            if claw_block == CLAW_BLOCKS:
                sum_claw()

            if 1 <= t < LAST:
                for half in range(HALVES):
                    project(t + 1, half)
            if piece:
                interleave_piece(piece[0], piece[1] + PIECES // 2)
            if 0 <= claw_block < CLAW_BLOCKS:
                for k in range(claw_block, claw_block + CLAW_PER_STEP):
                    add_claw_block(k)
            now = pair_pass(t, 3)
            if now:
                transpose_features(now[0], 2 * now[1])
                transpose_features(now[0], 2 * now[1] + 1)
            if HEAD_TILES <= t + AHEAD < N_TILES:
                transpose_tokens(t + AHEAD)

        last_pair = PAIRS[-1]
        single, final = (LAST - 1,), (LAST,)
        squared_deviations(LAST)
        inverse_deviation(LAST)
        normalise_at_once(LAST - 1)
        gain_and_shift(last_pair, 0)
        gain_and_shift(last_pair, 1)
        regroup_features(PAIRS[-2], 1)
        transpose_features(last_pair, 2)
        transpose_features(last_pair, 3)
        for g in range(PASSES):
            transpose_features(single, g)
        similarity(0, 0)
        quantise_features(PAIRS[-2], 1)
        gain_and_shift(last_pair, 2)
        gain_and_shift(last_pair, 3)
        normalise_at_once(LAST)
        for g in range(PASSES):
            gain_and_shift(single, g)
        regroup_features(last_pair, 0)
        similarity(0, 1)
        for g in range(PASSES):
            transpose_features(final, g)
        for g in range(PASSES):
            gain_and_shift(final, g)
        negated_logits(0, 0)
        quantise_features(last_pair, 0)
        regroup_features(last_pair, 1)
        negated_logits(0, 1)
        quantise_features(last_pair, 1)
        for g in range(PASSES):
            regroup_features(single, g)
        similarity(0, 2)
        similarity(0, 3)
        exponentials(0, 0)
        exponentials(0, 1)
        for g in range(PASSES):
            quantise_features(single, g)
        negated_logits(0, 2)
        for n in range(TILES_PER_UNIT - 1):
            similarity(1, n)
        for g in range(PASSES):
            regroup_features(final, g)
        negated_logits(0, 3)
        exponentials(0, 2)
        exponentials(0, 3)
        for g in range(PASSES):
            quantise_features(final, g)
        similarity(1, 3)
        invert_total(0, 0)
        negated_logits(1, 0)
        invert_total(0, 1)
        negated_logits(1, 1)
        store_probabilities(0, 0, "gpsimd")
        store_probabilities(0, 1, "gpsimd")
        exponentials(1, 0)
        exponentials(1, 1)
        invert_total(0, 2)
        negated_logits(1, 2)
        invert_total(0, 3)
        negated_logits(1, 3)
        store_probabilities(0, 2, "gpsimd")
        exponentials(1, 2)
        exponentials(1, 3)
        invert_total(1, 0)
        store_probabilities(0, 3)
        for n in range(TILES_PER_UNIT - 1):
            invert_total(1, n + 1)
            store_probabilities(1, n)
        store_probabilities(1, TILES_PER_UNIT - 1)
